import numpy as np
import ml_dtypes


def mxq(x, axis, fmt="e4m3"):
    dtype, down = {"e4m3": (ml_dtypes.float8_e4m3fn, 7), "e5m2": (ml_dtypes.float8_e5m2, 14)}[fmt]
    v = np.moveaxis(np.asarray(x, np.float32).astype(ml_dtypes.bfloat16).astype(np.float64), axis, -1)
    blocks = v.reshape(v.shape[:-1] + (-1, 32))
    amax = np.abs(blocks).max(-1, keepdims=True)
    byte = np.maximum(np.where(amax > 0, np.frexp(amax)[1] - 1 + 127, 0) - down, 1)
    scale = np.exp2(byte - 127.0)
    codes = (blocks / scale).astype(np.float32).astype(dtype).astype(np.float64)
    return np.moveaxis((codes * scale).reshape(v.shape), -1, axis)


WIDE = False


def mx_kscale(k):
    if not WIDE:
        return np.ones(k)
    levels = np.array([10, -10, 5, -5, 0])
    if k % 512:
        return np.exp2(np.random.permutation(np.resize(levels, k // 32))).repeat(32)
    a = np.empty((k // 512, 16))
    for p in range(k // 512):
        a[p, :8] = np.random.permutation(np.resize(levels, 8))
        for g in range(8):
            far = levels[np.abs(levels - a[p, g]) >= 10]
            a[p, g + 8] = far[np.random.randint(len(far))]
    return np.exp2(a.ravel()).repeat(32)


BF16 = ml_dtypes.bfloat16


def bf(x):
    return np.asarray(x, np.float32).astype(BF16)


def f64(x):
    return np.asarray(x).astype(np.float64)


E2M1 = np.array([0.0, 0.5, 1.0, 1.5, 2.0, 3.0, 4.0, 6.0, -0.0, -0.5, -1.0, -1.5, -2.0, -3.0, -4.0, -6.0])


def pack_weight(w, fmt):
    k, n = w.shape
    w = f64(bf(w)).reshape(k // 32, 32, n)
    amax = np.abs(w).max(1)
    if fmt == "e4m3":
        byte = np.frexp(amax)[1] - 1 + 127 - 7
    else:
        mant, ex = np.frexp(amax / 6.0)
        byte = np.where(mant > 0.5, ex, ex - 1) + 127
    byte = np.clip(np.where(amax > 0, byte, 1), 1, 254)
    scaled = (w * np.exp2(127.0 - byte)[:, None, :]).reshape(k, n).astype(np.float32)
    by_word = np.ascontiguousarray(scaled.reshape(k // 512, 128, 4, n).transpose(0, 1, 3, 2))
    if fmt == "e4m3":
        words = by_word.astype(ml_dtypes.float8_e4m3fn).view(np.uint8)
    else:
        c = by_word.astype(ml_dtypes.float4_e2m1fn).view(np.uint8) & 0xF
        words = c[..., 0::2] | (c[..., 1::2] << 4)
    return np.ascontiguousarray(words), np.ascontiguousarray(byte.astype(np.uint8).reshape(k // 512, 16, n))


def unpack_weight(words, scales, fmt):
    g, p, n, _ = words.shape
    if fmt == "e4m3":
        vals = np.ascontiguousarray(words).view(ml_dtypes.float8_e4m3fn).astype(np.float64)
    else:
        nib = np.empty((g, p, n, 4), np.uint8)
        nib[..., 0::2] = words & 0xF
        nib[..., 1::2] = words >> 4
        vals = E2M1[nib]
    vals = vals * np.repeat(np.exp2(scales.astype(np.float64) - 127.0), 8, axis=1)[..., None]
    return vals.transpose(0, 1, 3, 2).reshape(g * 512, n)
def pack4(w):
    words, scales = pack_weight(w, "e2m1")
    return words.reshape(words.shape[0], 128, -1), scales


def unpack4(words, scales):
    return unpack_weight(words.reshape(words.shape[0], 128, -1, 2), scales, "e2m1")


NB, DI, DO, B = 8, 1024, 1024, 256
F = NB * DO
EPS = 1e-5


def draw0():
    s, t = mx_kscale(DI), mx_kscale(F)
    tk = t.reshape(NB, DO)
    x = bf(np.random.standard_normal((B, DI)) * s)
    W = bf(np.random.standard_normal((NB, DI, DO)) / np.sqrt(DI) / s[None, :, None])
    b = bf(np.random.standard_normal((NB, DO)) * 0.5)
    gamma = bf((1.0 + 0.2 * np.random.standard_normal((NB, DO))) * tk)
    beta = bf(0.2 * np.random.standard_normal((NB, DO)) * tk)
    words, scales = pack4(np.random.standard_normal((F, DO)) / np.sqrt(F) / t[:, None])
    return {"x": x,
            "W": W,
            "b": b,
            "gamma": gamma,
            "beta": beta,
            "Wf1_words": words,
            "Wf1_scales": scales,
            "bf1": bf(np.random.standard_normal(DO) * 0.3)}


def core(x, W, b, gamma, beta, Wf1_words, Wf1_scales, bf1):
    w2 = f64(W).transpose(1, 0, 2).reshape(DI, F)
    h = (mxq(f64(x), 1, "e4m3") @ mxq(w2, 0, "e4m3")).reshape(B, NB, DO) + f64(b)[None]
    h = np.maximum(h, 0.0)
    mean = h.mean(axis=0, keepdims=True)
    var = ((h - mean) ** 2).mean(axis=0, keepdims=True)
    h = (h - mean) * (1.0 / np.sqrt(var + EPS)) * f64(gamma)[None] + f64(beta)[None]
    fused = h.reshape(B, F)
    return np.maximum((mxq(fused, 1, "e4m3") @ unpack4(Wf1_words, Wf1_scales)) + f64(bf1), 0.0)


def e4m3fn_bytes(y):
    return np.clip(np.asarray(y, np.float64), -448.0, 448.0).astype(np.float32).astype(ml_dtypes.float8_e4m3fn).view(np.uint8)


def e4m3fn_values(b):
    return np.asarray(b, np.uint8).view(ml_dtypes.float8_e4m3fn).astype(np.float64)


def setup_inputs():
    d = draw0()
    x0 = np.asarray(d['W']).astype(np.float64)
    s = (np.max(np.abs(x0), axis=(0, 2), keepdims=True) / 448.0).astype(np.float32)
    out = {}
    for k, v in d.items():
        if k == 'W':
            out['W_bytes'] = e4m3fn_bytes(x0 / s.astype(np.float64))
            out['W_scale'] = s
        else:
            out[k] = v
    return out


def reference(x, W_bytes, W_scale, b, gamma, beta, Wf1_words, Wf1_scales, bf1):
    return core(x, e4m3fn_values(W_bytes) * W_scale.astype(np.float64), b, gamma, beta, Wf1_words, Wf1_scales, bf1)

@@ -1,0 +1,269 @@
+from contextlib import ExitStack
+
+import concourse.mybir as mybir
+from concourse.masks import make_identity
+
+F32 = mybir.dt.float32
+BF16 = mybir.dt.bfloat16
+I32 = mybir.dt.int32
+U32 = mybir.dt.uint32
+U8 = mybir.dt.uint8
+FP8 = mybir.dt.float8_e4m3fn
+FP8X4 = mybir.dt.float8_e4m3fn_x4
+FP4X4 = mybir.dt.float4_e2m1fn_x4
+ACT = mybir.ActivationFunctionType
+ALU = mybir.AluOpType
+
+NB, DI, DO, B = 8, 1024, 1024, 256
+P = 128
+T = 4
+KP = P * T
+NG = DI // KP
+UNITS = NB * DO // KP
+EPS = 1e-5
+
+FLOPS = 2 * B * DI * NB * DO + 2 * B * NB * DO * DO
+
+
+def tile_extremeoptimizationlayer_pa_w4_kernel(tc, x, W_bytes, W_scale, b, gamma, beta, Wf1_words, Wf1_scales, bf1, out):
+    nc = tc.nc
+    with ExitStack() as ctx:
+        keep = ctx.enter_context(tc.tile_pool(name="keep", bufs=1))
+        wpool = ctx.enter_context(tc.tile_pool(name="wpool", bufs=4))
+        work = ctx.enter_context(tc.tile_pool(name="work", bufs=3))
+        hps = ctx.enter_context(tc.psum_pool(name="hps", bufs=4))
+        accps = ctx.enter_context(tc.psum_pool(name="accps", bufs=1))
+        ctx.enter_context(tc.manual_schedule())
+
+        warm = keep.tile([P, 1], F32, name="warm")
+        nc.vector.memset(warm[:], 1.0)
+        nc.scalar.activation(warm[:], warm[:], ACT.Sqrt)
+        eps = keep.tile([P, 1], F32, name="eps")
+        ident = keep.tile([P, P], F32, name="ident")
+        make_identity(nc, ident[:])
+        vrows = keep.tile([P, KP], BF16, name="vrows")
+        nc.vector.memset(vrows[:], 0.0)
+        nc.vector.memset(eps[:], 1.0)
+        nc.vector.tensor_scalar(eps[:], eps[:], EPS, None, op0=ALU.mult)
+
+        kscale = keep.tile([P, NG * T], F32, name="kscale")
+        nc.scalar.dma_start(out=kscale[:].rearrange("p (g t) -> p g t", g=NG), in_=W_scale.rearrange("o (g p t) z -> p (o g) (t z)", p=P, t=T))
+        for v, vec_in in enumerate((b, gamma, beta)):
+            nc.scalar.dma_start(out=vrows[16 * v : 16 * v + 16, :], in_=vec_in.rearrange("k (h c) -> (k h) c", c=KP))
+        x_sb = keep.tile([P, 2, DI], BF16, name="x_sb")
+
+        wbytes = {}
+
+        def load_first_branch():
+            src = W_bytes[0].rearrange("(g p t) o -> p g t o", p=P, t=T)
+            for half in range(2):
+                wb = keep.tile([P, NG, T, KP], U8, name="wb0%d" % half)
+                for g in range(NG):
+                    nc.sync.dma_start(out=wb[:, g], in_=src[:, g, :, half * KP : (half + 1) * KP])
+                    if half == 0 and g == 0:
+                        nc.sync.dma_start(out=x_sb[:], in_=x.rearrange("(r p) k -> p r k", p=P))
+                wbytes[half] = wb
+
+        def load_branch(k):
+            wb = wpool.tile([P, NG, T, DO], U8, name="wb")
+            src = W_bytes[k].rearrange("(g p t) o -> p g t o", p=P, t=T)
+            for g in range(NG):
+                nc.sync.dma_start(out=wb[:, g], in_=src[:, g])
+            for half in range(2):
+                wbytes[2 * k + half] = wb[:, :, :, half * KP : (half + 1) * KP]
+
+        load_first_branch()
+        load_branch(1)
+
+        wf = keep.tile([P, UNITS, 2 * DO], U8, name="wf", align_bytes=64)
+        wfs = keep.tile([P, UNITS, DO], U8, name="wfs", align_bytes=64)
+        nc.gpsimd.memset(wfs[:].rearrange("p u n -> p (u n)").bitcast(I32), 0)
+        for q in range(4):
+            nc.sync.dma_start(
+                out=wfs[32 * q : 32 * q + 4].bitcast(I32),
+                in_=Wf1_scales[:, 4 * q : 4 * q + 4, :].rearrange("u q n -> q u n").bitcast(I32),
+            )
+        nc.sync.dma_start(out=wf[:, 0:4], in_=Wf1_words[0:4].rearrange("u p n -> p u n"))
+        load_branch(2)
+        load_branch(3)
+        bf1_b = keep.tile([P, DO], BF16, name="bf1_b")
+
+        x_codes = keep.tile([P, NG, B], U32, name="x_codes", align_bytes=64)
+        x_scales = keep.tile([P, NG, B], U8, name="x_scales", align_bytes=64)
+        x_words = x_sb[:].bitcast(F32)
+        x_grouped = []
+        for g in range(NG):
+            xt = hps.tile([P, 2, 2, P], F32, name="h")
+            for r in range(2):
+                for u in range(2):
+                    nc.tensor.transpose(xt[:, r, u, :], x_words[:, r, 256 * g + u : 256 * (g + 1) : 2], ident[:])
+            xg = keep.tile([P, B, T], BF16, name="xg%d" % g, align_bytes=64)
+            dst = xg[:].bitcast(F32).rearrange("p (r n) u -> p r n u", r=2)
+            src = xt[:].rearrange("p r u n -> p r n u")
+            if g == 0:
+                nc.scalar.copy(dst, src)
+            else:
+                nc.scalar.copy(dst, src)
+            x_grouped.append(xg)
+        vt = hps.tile([P, 2, 2, P], F32, name="h")
+        for u in range(2):
+            nc.tensor.transpose(vt[:, 0, u, :], vrows[:].bitcast(F32)[:, u::2], ident[:])
+        vec16 = keep.tile([P, 48, T], BF16, name="vec16")
+        nc.scalar.copy(vec16[:].bitcast(F32), vt[:, 0, :, 0:48].rearrange("p u r -> p r u"))
+        vec = keep.tile([P, 48, T], F32, name="vec")
+        nc.scalar.copy(vec[:], vec16[:])
+
+        act_codes = keep.tile([P, UNITS, B], U32, name="act_codes", align_bytes=64)
+        act_scales = keep.tile([P, UNITS, B], U8, name="act_scales", align_bytes=64)
+        acc = {}
+        for m in range(2):
+            for n in range(2):
+                acc[m, n] = accps.tile([P, KP], F32, name="acc%d%d" % (m, n))
+
+        plane, grouped, codes, scales = {}, {}, {}, {}
+        h, a, stat, sq, shift, nplane, ngrp = {}, {}, {}, {}, {}, {}, {}
+
+        def widen(i, g):
+            wb = wbytes[i]
+            plane[i, g] = work.tile([P, 2, KP, 2], BF16, name="plane", align_bytes=64)
+            for t in range(T):
+                nc.vector.tensor_scalar(
+                    plane[i, g][:, t // 2, :, t % 2], wb[:, g, t, :].bitcast(FP8), kscale[:, g * T + t : g * T + t + 1], None, op0=ALU.mult
+                )
+
+        def merge(i, g):
+            grouped[i, g] = work.tile([P, KP, T], BF16, name="grouped", align_bytes=64)
+            dst = grouped[i, g][:].rearrange("p c j -> p (c j)").bitcast(F32).rearrange("p (t m u) -> p m t u", t=T, u=2)
+            src = plane[i, g][:].rearrange("p u c e -> p (u c e)").bitcast(F32).rearrange("p (u m t) -> p m t u", u=2, t=T)
+            nc.scalar.copy(dst, src)
+
+        def quant(i, g):
+            if g == 0:
+                codes[i] = work.tile([P, NG, KP], U32, name="codes", align_bytes=64)
+                scales[i] = work.tile([P, NG, KP], U8, name="scales", align_bytes=64)
+            nc.vector.quantize_mx(codes[i][:, g, :].bitcast(FP8X4), scales[i][:, g, :], grouped[i, g][:].rearrange("p c j -> p (c j)"))
+
+        def mm1(i):
+            for half in range(2):
+                h[i, half] = hps.tile([P, 2, B], F32, name="h")
+                for s in range(2):
+                    c = slice(P * (2 * half + s), P * (2 * half + s + 1))
+                    for g in range(NG):
+                        nc.tensor.matmul_mx(
+                            h[i, half][:, s, :],
+                            lhsT=codes[i][:, g, c].bitcast(FP8X4),
+                            lhsT_scale=scales[i][:, g, c],
+                            rhs=x_codes[:, g, :].bitcast(FP8X4),
+                            rhs_scale=x_scales[:, g, :],
+                            start=(g == 0),
+                            stop=(g == NG - 1),
+                        )
+
+        def relu(i, half):
+            if half == 0:
+                a[i] = work.tile([P, T, B], F32, name="a")
+                stat[i] = work.tile([P, T], F32, name="stat")
+            for s in range(2):
+                t = 2 * half + s
+                nc.scalar.activation(a[i][:, t, :], h[i, half][:, s, :], ACT.Relu, bias=vec[:, i, t : t + 1], accum_out=stat[i][:, t : t + 1])
+
+        def center(i):
+            shift[i] = work.tile([P, T], F32, name="shift")
+            nc.vector.tensor_scalar(shift[i][:], stat[i][:], -1.0 / B, None, op0=ALU.mult)
+            sq[i] = work.tile([P, T], F32, name="sq")
+
+        def square(i, half):
+            for t in (2 * half, 2 * half + 1):
+                junk = work.tile([P, B], BF16, name="junk")
+                nc.scalar.activation(junk[:], a[i][:, t, :], ACT.Square, bias=shift[i][:, t : t + 1], accum_out=sq[i][:, t : t + 1])
+
+        scl, off = {}, {}
+
+        def root(i):
+            std = work.tile([P, T], F32, name="std")
+            nc.scalar.activation(std[:], sq[i][:], ACT.Sqrt, bias=eps[:], scale=1.0 / B)
+            sq[i] = std
+
+        def coeff(i):
+            rs = work.tile([P, T], F32, name="rs")
+            nc.vector.reciprocal(rs[:], sq[i][:])
+            scl[i] = work.tile([P, T], F32, name="scl")
+            off[i] = work.tile([P, T], F32, name="off")
+            tmp = work.tile([P, T], F32, name="tmp")
+            nc.vector.tensor_tensor(scl[i][:], rs[:], vec[:, 16 + i, :], op=ALU.mult)
+            nc.vector.tensor_tensor(tmp[:], shift[i][:], scl[i][:], op=ALU.mult)
+            nc.vector.tensor_tensor(off[i][:], tmp[:], vec[:, 32 + i, :], op=ALU.add)
+
+        def norm(i):
+            nplane[i] = work.tile([P, 2, B, 2], BF16, name="nplane", align_bytes=64)
+            for t in range(T):
+                nc.vector.tensor_scalar(
+                    nplane[i][:, t // 2, :, t % 2], a[i][:, t, :], scl[i][:, t : t + 1], off[i][:, t : t + 1], op0=ALU.mult, op1=ALU.add
+                )
+
+        def nmerge(i):
+            ngrp[i] = work.tile([P, B, T], BF16, name="ngrp", align_bytes=64)
+            nc.scalar.copy(
+                ngrp[i][:].rearrange("p n t -> p (n t)").bitcast(F32).rearrange("p (n u) -> p n u", u=2),
+                nplane[i][:].rearrange("p u n e -> p (u n e)").bitcast(F32).rearrange("p (u n) -> p n u", u=2),
+            )
+
+        def nquant(i):
+            nc.vector.quantize_mx(act_codes[:, i, :].bitcast(FP8X4), act_scales[:, i, :], ngrp[i][:].rearrange("p n t -> p (n t)"))
+
+        def mm2(i):
+            for m in range(2):
+                rows = slice(P * m, P * (m + 1))
+                for n in range(2):
+                    nc.tensor.matmul_mx(
+                        acc[m, n][:],
+                        lhsT=act_codes[:, i, rows].bitcast(FP8X4),
+                        lhsT_scale=act_scales[:, i, rows],
+                        rhs=wf[:, i, DO * n : DO * (n + 1)].bitcast(FP4X4),
+                        rhs_scale=wfs[:, i, KP * n : KP * (n + 1)],
+                        start=(i == 0),
+                        stop=(i == UNITS - 1),
+                    )
+
+        def when(f, i, *args):
+            if 0 <= i < UNITS:
+                f(i, *args)
+
+        for s in range(UNITS + 3):
+            if s % 2 == 0 and 4 <= s // 2 + 3 < NB:
+                load_branch(s // 2 + 3)
+                if s // 2 <= 3:
+                    u = slice(4 * (s // 2), 4 * (s // 2) + 4)
+                    nc.sync.dma_start(out=wf[:, u], in_=Wf1_words[u].rearrange("u p n -> p u n"))
+            if s == 4:
+                nc.sync.dma_start(out=bf1_b[:], in_=bf1.partition_broadcast(P))
+            when(widen, s, 0)
+            if s == 0:
+                for g in range(NG):
+                    nc.vector.quantize_mx(x_codes[:, g, :].bitcast(FP8X4), x_scales[:, g, :], x_grouped[g][:].rearrange("p n t -> p (n t)"))
+            when(nmerge, s - 3)
+            when(square, s - 2, 0)
+            when(square, s - 2, 1)
+            when(root, s - 2)
+            when(merge, s, 0)
+            when(quant, s - 1, 1)
+            when(mm1, s - 1)
+            when(nquant, s - 3)
+            when(widen, s, 1)
+            when(relu, s - 1, 0)
+            when(relu, s - 1, 1)
+            when(quant, s, 0)
+            when(coeff, s - 2)
+            when(norm, s - 2)
+            when(center, s - 1)
+            when(merge, s, 1)
+            when(mm2, s - 3)
+
+        for m in range(2):
+            for n in range(2):
+                z = work.tile([P, KP], F32, name="z")
+                cols = slice(KP * n, KP * (n + 1))
+                nc.vector.tensor_tensor(z[:], acc[m, n][:], bf1_b[:, cols], op=ALU.add)
+                o = work.tile([P, KP], F32, name="o")
+                nc.scalar.activation(o[:], z[:], ACT.Relu)
+                nc.sync.dma_start(out=out[P * m : P * (m + 1), cols], in_=o[:])

@@ -21,6 +21,7 @@ KP = P * T
 NG = DI // KP
 UNITS = NB * DO // KP
 EPS = 1e-5
+WOVEN = ((0, 32, 64), (64, 96, 102))
 
 FLOPS = 2 * B * DI * NB * DO + 2 * B * NB * DO * DO
 
@@ -29,119 +30,145 @@ def tile_extremeoptimizationlayer_pa_w4_kernel(tc, x, W_bytes, W_scale, b, gamma
     nc = tc.nc
     with ExitStack() as ctx:
         keep = ctx.enter_context(tc.tile_pool(name="keep", bufs=1))
-        wpool = ctx.enter_context(tc.tile_pool(name="wpool", bufs=4))
-        work = ctx.enter_context(tc.tile_pool(name="work", bufs=3))
-        hps = ctx.enter_context(tc.psum_pool(name="hps", bufs=4))
+        work = ctx.enter_context(tc.tile_pool(name="work", bufs=2))
+        deep = ctx.enter_context(tc.tile_pool(name="deep", bufs=3))
+        hps = ctx.enter_context(tc.psum_pool(name="hps", bufs=2))
+        wps = ctx.enter_context(tc.psum_pool(name="wps", bufs=2))
         accps = ctx.enter_context(tc.psum_pool(name="accps", bufs=1))
         ctx.enter_context(tc.manual_schedule())
 
-        warm = keep.tile([P, 1], F32, name="warm")
-        nc.vector.memset(warm[:], 1.0)
-        nc.scalar.activation(warm[:], warm[:], ACT.Sqrt)
-        eps = keep.tile([P, 1], F32, name="eps")
-        ident = keep.tile([P, P], F32, name="ident")
-        make_identity(nc, ident[:])
-        vrows = keep.tile([P, KP], BF16, name="vrows")
-        nc.vector.memset(vrows[:], 0.0)
-        nc.vector.memset(eps[:], 1.0)
-        nc.vector.tensor_scalar(eps[:], eps[:], EPS, None, op0=ALU.mult)
-
         kscale = keep.tile([P, NG * T], F32, name="kscale")
         nc.scalar.dma_start(out=kscale[:].rearrange("p (g t) -> p g t", g=NG), in_=W_scale.rearrange("o (g p t) z -> p (o g) (t z)", p=P, t=T))
+        vrows = keep.tile([P, KP], BF16, name="vrows")
+        nc.vector.memset(vrows[:], 0.0)
         for v, vec_in in enumerate((b, gamma, beta)):
             nc.scalar.dma_start(out=vrows[16 * v : 16 * v + 16, :], in_=vec_in.rearrange("k (h c) -> (k h) c", c=KP))
-        x_sb = keep.tile([P, 2, DI], BF16, name="x_sb")
 
         wbytes = {}
 
-        def load_first_branch():
-            src = W_bytes[0].rearrange("(g p t) o -> p g t o", p=P, t=T)
-            for half in range(2):
-                wb = keep.tile([P, NG, T, KP], U8, name="wb0%d" % half)
-                for g in range(NG):
-                    nc.sync.dma_start(out=wb[:, g], in_=src[:, g, :, half * KP : (half + 1) * KP])
-                    if half == 0 and g == 0:
-                        nc.sync.dma_start(out=x_sb[:], in_=x.rearrange("(r p) k -> p r k", p=P))
-                wbytes[half] = wb
+        def load_w(k, g, halves):
+            src = W_bytes[k].rearrange("(g p t) o -> g p t o", p=P, t=T)[g]
+            cols = slice(KP * halves[0], KP * (halves[-1] + 1))
+            wb = keep.tile([P, T, KP * len(halves)], U8, name="wb%d_%d_%d" % (k, g, halves[0]))
+            nc.sync.dma_start(out=wb[:], in_=src[:, :, cols])
+            for n, half in enumerate(halves):
+                wbytes[2 * k + half, g] = wb[:, :, KP * n : KP * (n + 1)]
 
-        def load_branch(k):
-            wb = wpool.tile([P, NG, T, DO], U8, name="wb")
-            src = W_bytes[k].rearrange("(g p t) o -> p g t o", p=P, t=T)
-            for g in range(NG):
-                nc.sync.dma_start(out=wb[:, g], in_=src[:, g])
-            for half in range(2):
-                wbytes[2 * k + half] = wb[:, :, :, half * KP : (half + 1) * KP]
-
-        load_first_branch()
-        load_branch(1)
-
+        x_sb = keep.tile([P, 2, DI], BF16, name="x_sb")
         wf = keep.tile([P, UNITS, 2 * DO], U8, name="wf", align_bytes=64)
         wfs = keep.tile([P, UNITS, DO], U8, name="wfs", align_bytes=64)
-        nc.gpsimd.memset(wfs[:].rearrange("p u n -> p (u n)").bitcast(I32), 0)
+        bf1_b = keep.tile([P, DO], BF16, name="bf1_b")
+
+        load_w(0, 1, (0,))
+        load_w(0, 0, (0,))
+        nc.sync.dma_start(out=x_sb[:], in_=x.rearrange("(r p) k -> p r k", p=P))
+        load_w(0, 1, (1,))
+        load_w(0, 0, (1,))
+        load_w(1, 1, (0, 1))
+        load_w(1, 0, (0, 1))
+
+        ident = keep.tile([P, P], F32, name="ident")
+        make_identity(nc, ident[:])
+        ident16 = keep.tile([P, P], BF16, name="ident16")
+        make_identity(nc, ident16[:])
+        eps = keep.tile([P, 1], F32, name="eps")
+        nc.vector.memset(eps[:], 1.0)
+        for q in range(4):
+            nc.vector.memset(wfs[:, 4 * q : 4 * q + 4, :].rearrange("p u n -> p (u n)").bitcast(I32), 0)
+        nc.vector.tensor_scalar(eps[:], eps[:], EPS, None, op0=ALU.mult)
+
         for q in range(4):
             nc.sync.dma_start(
                 out=wfs[32 * q : 32 * q + 4].bitcast(I32),
                 in_=Wf1_scales[:, 4 * q : 4 * q + 4, :].rearrange("u q n -> q u n").bitcast(I32),
             )
-        nc.sync.dma_start(out=wf[:, 0:4], in_=Wf1_words[0:4].rearrange("u p n -> p u n"))
-        load_branch(2)
-        load_branch(3)
-        bf1_b = keep.tile([P, DO], BF16, name="bf1_b")
+        for k in range(2, NB):
+            if k - 2 < 4:
+                u = slice(4 * (k - 2), 4 * (k - 2) + 4)
+                nc.sync.dma_start(out=wf[:, u], in_=Wf1_words[u].rearrange("u p n -> p u n"))
+            load_w(k, 1, (0, 1))
+            load_w(k, 0, (0, 1))
+        nc.sync.dma_start(out=bf1_b[:], in_=bf1.partition_broadcast(P))
 
         x_codes = keep.tile([P, NG, B], U32, name="x_codes", align_bytes=64)
         x_scales = keep.tile([P, NG, B], U8, name="x_scales", align_bytes=64)
-        x_words = x_sb[:].bitcast(F32)
-        x_grouped = []
-        for g in range(NG):
-            xt = hps.tile([P, 2, 2, P], F32, name="h")
-            for r in range(2):
-                for u in range(2):
-                    nc.tensor.transpose(xt[:, r, u, :], x_words[:, r, 256 * g + u : 256 * (g + 1) : 2], ident[:])
-            xg = keep.tile([P, B, T], BF16, name="xg%d" % g, align_bytes=64)
-            dst = xg[:].bitcast(F32).rearrange("p (r n) u -> p r n u", r=2)
-            src = xt[:].rearrange("p r u n -> p r n u")
-            if g == 0:
-                nc.scalar.copy(dst, src)
-            else:
-                nc.scalar.copy(dst, src)
-            x_grouped.append(xg)
-        vt = hps.tile([P, 2, 2, P], F32, name="h")
-        for u in range(2):
-            nc.tensor.transpose(vt[:, 0, u, :], vrows[:].bitcast(F32)[:, u::2], ident[:])
-        vec16 = keep.tile([P, 48, T], BF16, name="vec16")
-        nc.scalar.copy(vec16[:].bitcast(F32), vt[:, 0, :, 0:48].rearrange("p u r -> p r u"))
-        vec = keep.tile([P, 48, T], F32, name="vec")
-        nc.scalar.copy(vec[:], vec16[:])
+        x_grouped = keep.tile([P, NG, B, T], BF16, name="x_grouped", align_bytes=64)
+        vec = keep.tile([P, 3 * UNITS, T], F32, name="vec")
 
-        act_codes = keep.tile([P, UNITS, B], U32, name="act_codes", align_bytes=64)
-        act_scales = keep.tile([P, UNITS, B], U8, name="act_scales", align_bytes=64)
+        def turn_x():
+            x_words = x_sb[:].bitcast(F32)
+            for g in range(NG):
+                xt = hps.tile([P, 2, 2, P], F32, name="h")
+                for r in range(2):
+                    for u in range(2):
+                        nc.tensor.transpose(xt[:, r, u, :], x_words[:, r, 256 * g + u : 256 * (g + 1) : 2], ident[:])
+                dst = x_grouped[:, g].bitcast(F32).rearrange("p (r n) u -> p r n u", r=2)
+                nc.scalar.copy(dst, xt[:].rearrange("p r u n -> p r n u"))
+
+        def turn_vectors():
+            vt = hps.tile([P, 2, P], F32, name="h")
+            for u in range(2):
+                nc.tensor.transpose(vt[:, u, :], vrows[:].bitcast(F32)[:, u::2], ident[:])
+            halves = vt[:].bitcast(BF16).rearrange("p u (r e) -> p r u e", e=2)
+            for v, factor in enumerate((1.0 / B, float(B), 1.0)):
+                rows = slice(UNITS * v, UNITS * (v + 1))
+                nc.scalar.activation(vec[:, rows, :].rearrange("p r (u e) -> p r u e", e=2), halves[:, rows], ACT.Copy, scale=factor)
+
+        def quant_x():
+            nc.vector.quantize_mx(
+                x_codes[:].rearrange("p g n -> p (g n)").bitcast(FP8X4),
+                x_scales[:].rearrange("p g n -> p (g n)"),
+                x_grouped[:].rearrange("p g n t -> p (g n t)"),
+            )
+
         acc = {}
         for m in range(2):
             for n in range(2):
                 acc[m, n] = accps.tile([P, KP], F32, name="acc%d%d" % (m, n))
 
-        plane, grouped, codes, scales = {}, {}, {}, {}
-        h, a, stat, sq, shift, nplane, ngrp = {}, {}, {}, {}, {}, {}, {}
+        plane, grouped, woven, codes, scales = {}, {}, {}, {}, {}
+        h, a, mean, sq, std, scl, off, tmp, nplane, ngrp, act_codes, act_scales = ({} for n in range(12))
 
-        def widen(i, g):
-            wb = wbytes[i]
-            plane[i, g] = work.tile([P, 2, KP, 2], BF16, name="plane", align_bytes=64)
-            for t in range(T):
+        def widen(i, g, rows):
+            if (i, g) not in plane:
+                plane[i, g] = work.tile([P, T, KP], BF16, name="plane%d" % g, align_bytes=64)
+            for j in rows:
                 nc.vector.tensor_scalar(
-                    plane[i, g][:, t // 2, :, t % 2], wb[:, g, t, :].bitcast(FP8), kscale[:, g * T + t : g * T + t + 1], None, op0=ALU.mult
+                    plane[i, g][:, j, :], wbytes[i, g][:, j, :].bitcast(FP8), kscale[:, g * T + j : g * T + j + 1], None, op0=ALU.mult
                 )
 
-        def merge(i, g):
-            grouped[i, g] = work.tile([P, KP, T], BF16, name="grouped", align_bytes=64)
-            dst = grouped[i, g][:].rearrange("p c j -> p (c j)").bitcast(F32).rearrange("p (t m u) -> p m t u", t=T, u=2)
-            src = plane[i, g][:].rearrange("p u c e -> p (u c e)").bitcast(F32).rearrange("p (u m t) -> p m t u", u=2, t=T)
-            nc.scalar.copy(dst, src)
+        def group_tile(i, g):
+            if (i, g) not in grouped:
+                grouped[i, g] = work.tile([P, T, P, T], BF16, name="grouped%d" % g, align_bytes=64)
+            return grouped[i, g]
+
+        def lay_out(copy, i, g, m0, m1):
+            dst = group_tile(i, g)[:, :, m0:m1, :].rearrange("p t (q e) j -> p q t j e", e=2)
+            src = plane[i, g][:, :, T * m0 : T * m1].rearrange("p j (q e t) -> p q t j e", e=2, t=T)
+            copy(dst, src)
+
+        def weave(i):
+            for bank, cuts in enumerate(WOVEN):
+                quads = cuts[-1] - cuts[0]
+                woven[i, bank] = wps.tile([P, T, quads, T], BF16, name="woven")
+                for m0, m1 in zip(cuts[:-1], cuts[1:]):
+                    nc.tensor.matmul(
+                        woven[i, bank][:, :, m0 - cuts[0] : m1 - cuts[0], :].rearrange("p t m j -> p m t j"),
+                        lhsT=ident16[:],
+                        rhs=plane[i, 1][:, :, T * m0 : T * m1].rearrange("p j (m t) -> p m t j", t=T),
+                        start=True,
+                        stop=True,
+                    )
+
+        def unweave(i):
+            for bank, cuts in enumerate(WOVEN):
+                nc.scalar.copy(group_tile(i, 1)[:, :, cuts[0] : cuts[-1], :], woven[i, bank][:])
+            lay_out(nc.scalar.copy, i, 1, WOVEN[-1][-1], P)
 
         def quant(i, g):
-            if g == 0:
-                codes[i] = work.tile([P, NG, KP], U32, name="codes", align_bytes=64)
-                scales[i] = work.tile([P, NG, KP], U8, name="scales", align_bytes=64)
-            nc.vector.quantize_mx(codes[i][:, g, :].bitcast(FP8X4), scales[i][:, g, :], grouped[i, g][:].rearrange("p c j -> p (c j)"))
+            codes[i, g] = work.tile([P, KP], U32, name="codes%d" % g, align_bytes=64)
+            scales[i, g] = work.tile([P, KP], U8, name="scales%d" % g, align_bytes=64)
+            nc.vector.quantize_mx(codes[i, g][:].bitcast(FP8X4), scales[i, g][:], grouped[i, g][:].rearrange("p t m j -> p (t m j)"))
 
         def mm1(i):
             for half in range(2):
@@ -151,65 +178,61 @@ def tile_extremeoptimizationlayer_pa_w4_kernel(tc, x, W_bytes, W_scale, b, gamma
                     for g in range(NG):
                         nc.tensor.matmul_mx(
                             h[i, half][:, s, :],
-                            lhsT=codes[i][:, g, c].bitcast(FP8X4),
-                            lhsT_scale=scales[i][:, g, c],
+                            lhsT=codes[i, g][:, c].bitcast(FP8X4),
+                            lhsT_scale=scales[i, g][:, c],
                             rhs=x_codes[:, g, :].bitcast(FP8X4),
                             rhs_scale=x_scales[:, g, :],
                             start=(g == 0),
                             stop=(g == NG - 1),
                         )
 
-        def relu(i, half):
-            if half == 0:
-                a[i] = work.tile([P, T, B], F32, name="a")
-                stat[i] = work.tile([P, T], F32, name="stat")
-            for s in range(2):
-                t = 2 * half + s
-                nc.scalar.activation(a[i][:, t, :], h[i, half][:, s, :], ACT.Relu, bias=vec[:, i, t : t + 1], accum_out=stat[i][:, t : t + 1])
+        def relu(i):
+            a[i] = deep.tile([P, T, B], F32, name="a")
+            mean[i] = deep.tile([P, T], F32, name="mean")
+            for t in range(T):
+                nc.scalar.activation(
+                    a[i][:, t, :], h[i, t // 2][:, t % 2, :], ACT.Relu, bias=vec[:, i, t : t + 1], scale=1.0 / B, accum_out=mean[i][:, t : t + 1]
+                )
 
-        def center(i):
-            shift[i] = work.tile([P, T], F32, name="shift")
-            nc.vector.tensor_scalar(shift[i][:], stat[i][:], -1.0 / B, None, op0=ALU.mult)
+        def square(i):
             sq[i] = work.tile([P, T], F32, name="sq")
-
-        def square(i, half):
-            for t in (2 * half, 2 * half + 1):
-                junk = work.tile([P, B], BF16, name="junk")
-                nc.scalar.activation(junk[:], a[i][:, t, :], ACT.Square, bias=shift[i][:, t : t + 1], accum_out=sq[i][:, t : t + 1])
-
-        scl, off = {}, {}
+            junk = work.tile([P, T, B], BF16, name="junk")
+            for t in range(T):
+                nc.scalar.activation(
+                    junk[:, t, :], a[i][:, t, :], ACT.Square, bias=mean[i][:, t : t + 1], scale=-float(B), accum_out=sq[i][:, t : t + 1]
+                )
 
         def root(i):
-            std = work.tile([P, T], F32, name="std")
-            nc.scalar.activation(std[:], sq[i][:], ACT.Sqrt, bias=eps[:], scale=1.0 / B)
-            sq[i] = std
+            std[i] = work.tile([P, T], F32, name="std")
+            nc.scalar.activation(std[i][:], sq[i][:], ACT.Sqrt, bias=eps[:], scale=1.0 / B)
 
-        def coeff(i):
-            rs = work.tile([P, T], F32, name="rs")
-            nc.vector.reciprocal(rs[:], sq[i][:])
-            scl[i] = work.tile([P, T], F32, name="scl")
-            off[i] = work.tile([P, T], F32, name="off")
-            tmp = work.tile([P, T], F32, name="tmp")
-            nc.vector.tensor_tensor(scl[i][:], rs[:], vec[:, 16 + i, :], op=ALU.mult)
-            nc.vector.tensor_tensor(tmp[:], shift[i][:], scl[i][:], op=ALU.mult)
-            nc.vector.tensor_tensor(off[i][:], tmp[:], vec[:, 32 + i, :], op=ALU.add)
+        def coeff(i, stage):
+            if stage == 0:
+                tmp[i] = work.tile([P, T], F32, name="rstd")
+                nc.vector.reciprocal(tmp[i][:], std[i][:])
+            if stage == 1:
+                scl[i] = work.tile([P, T], F32, name="scl")
+                nc.vector.tensor_tensor(scl[i][:], tmp[i][:], vec[:, UNITS + i, :], op=ALU.mult)
+            if stage == 2:
+                tmp[i] = work.tile([P, T], F32, name="shift")
+                nc.vector.scalar_tensor_tensor(tmp[i][:], mean[i][:], -1.0 / B, scl[i][:], op0=ALU.mult, op1=ALU.mult)
+            if stage == 3:
+                off[i] = work.tile([P, T], F32, name="off")
+                nc.vector.tensor_tensor(off[i][:], tmp[i][:], vec[:, 2 * UNITS + i, :], op=ALU.add)
 
         def norm(i):
-            nplane[i] = work.tile([P, 2, B, 2], BF16, name="nplane", align_bytes=64)
+            nplane[i] = work.tile([P, T, B], BF16, name="nplane", align_bytes=64)
             for t in range(T):
-                nc.vector.tensor_scalar(
-                    nplane[i][:, t // 2, :, t % 2], a[i][:, t, :], scl[i][:, t : t + 1], off[i][:, t : t + 1], op0=ALU.mult, op1=ALU.add
-                )
+                nc.vector.tensor_scalar(nplane[i][:, t, :], a[i][:, t, :], scl[i][:, t : t + 1], off[i][:, t : t + 1], op0=ALU.mult, op1=ALU.add)
 
         def nmerge(i):
             ngrp[i] = work.tile([P, B, T], BF16, name="ngrp", align_bytes=64)
-            nc.scalar.copy(
-                ngrp[i][:].rearrange("p n t -> p (n t)").bitcast(F32).rearrange("p (n u) -> p n u", u=2),
-                nplane[i][:].rearrange("p u n e -> p (u n e)").bitcast(F32).rearrange("p (u n) -> p n u", u=2),
-            )
+            nc.scalar.copy(ngrp[i][:].rearrange("p (c e) t -> p c t e", e=2), nplane[i][:].rearrange("p t (c e) -> p c t e", e=2))
 
         def nquant(i):
-            nc.vector.quantize_mx(act_codes[:, i, :].bitcast(FP8X4), act_scales[:, i, :], ngrp[i][:].rearrange("p n t -> p (n t)"))
+            act_codes[i] = work.tile([P, B], U32, name="act_codes", align_bytes=64)
+            act_scales[i] = work.tile([P, B], U8, name="act_scales", align_bytes=64)
+            nc.vector.quantize_mx(act_codes[i][:].bitcast(FP8X4), act_scales[i][:], ngrp[i][:].rearrange("p n t -> p (n t)"))
 
         def mm2(i):
             for m in range(2):
@@ -217,8 +240,8 @@ def tile_extremeoptimizationlayer_pa_w4_kernel(tc, x, W_bytes, W_scale, b, gamma
                 for n in range(2):
                     nc.tensor.matmul_mx(
                         acc[m, n][:],
-                        lhsT=act_codes[:, i, rows].bitcast(FP8X4),
-                        lhsT_scale=act_scales[:, i, rows],
+                        lhsT=act_codes[i][:, rows].bitcast(FP8X4),
+                        lhsT_scale=act_scales[i][:, rows],
                         rhs=wf[:, i, DO * n : DO * (n + 1)].bitcast(FP4X4),
                         rhs_scale=wfs[:, i, KP * n : KP * (n + 1)],
                         start=(i == 0),
@@ -229,35 +252,32 @@ def tile_extremeoptimizationlayer_pa_w4_kernel(tc, x, W_bytes, W_scale, b, gamma
             if 0 <= i < UNITS:
                 f(i, *args)
 
+        def lay_out_pass0(i):
+            lay_out(nc.scalar.copy if i < 2 else nc.vector.tensor_copy, i, 0, 0, P)
+
         for s in range(UNITS + 3):
-            if s % 2 == 0 and 4 <= s // 2 + 3 < NB:
-                load_branch(s // 2 + 3)
-                if s // 2 <= 3:
-                    u = slice(4 * (s // 2), 4 * (s // 2) + 4)
-                    nc.sync.dma_start(out=wf[:, u], in_=Wf1_words[u].rearrange("u p n -> p u n"))
-            if s == 4:
-                nc.sync.dma_start(out=bf1_b[:], in_=bf1.partition_broadcast(P))
-            when(widen, s, 0)
+            when(widen, s, 1, range(T))
             if s == 0:
-                for g in range(NG):
-                    nc.vector.quantize_mx(x_codes[:, g, :].bitcast(FP8X4), x_scales[:, g, :], x_grouped[g][:].rearrange("p n t -> p (n t)"))
-            when(nmerge, s - 3)
-            when(square, s - 2, 0)
-            when(square, s - 2, 1)
+                turn_x()
+                turn_vectors()
+            when(square, s - 2)
             when(root, s - 2)
-            when(merge, s, 0)
+            when(weave, s)
+            when(quant, s - 1, 0)
             when(quant, s - 1, 1)
             when(mm1, s - 1)
+            when(nmerge, s - 3)
+            for j in range(T):
+                when(widen, s, 0, (j,))
+                when(coeff, s - 2, j)
+            if s == 0:
+                quant_x()
+            when(unweave, s)
             when(nquant, s - 3)
-            when(widen, s, 1)
-            when(relu, s - 1, 0)
-            when(relu, s - 1, 1)
-            when(quant, s, 0)
-            when(coeff, s - 2)
-            when(norm, s - 2)
-            when(center, s - 1)
-            when(merge, s, 1)
             when(mm2, s - 3)
+            when(norm, s - 2)
+            when(relu, s - 1)
+            when(lay_out_pass0, s)
 
         for m in range(2):
             for n in range(2):

@@ -20,8 +20,9 @@ T = 4
 KP = P * T
 NG = DI // KP
 UNITS = NB * DO // KP
+LAST = UNITS - 1
 EPS = 1e-5
-WOVEN = ((0, 32, 64), (64, 96, 102))
+COPIED, PAIRED = 2, 4
 
 FLOPS = 2 * B * DI * NB * DO + 2 * B * NB * DO * DO
 
@@ -73,9 +74,9 @@ def tile_extremeoptimizationlayer_pa_w4_kernel(tc, x, W_bytes, W_scale, b, gamma
         make_identity(nc, ident16[:])
         eps = keep.tile([P, 1], F32, name="eps")
         nc.vector.memset(eps[:], 1.0)
+        nc.scalar.activation(eps[:], eps[:], ACT.Abs_reciprocal_sqrt, scale=EPS**-2)
         for q in range(4):
             nc.vector.memset(wfs[:, 4 * q : 4 * q + 4, :].rearrange("p u n -> p (u n)").bitcast(I32), 0)
-        nc.vector.tensor_scalar(eps[:], eps[:], EPS, None, op0=ALU.mult)
 
         for q in range(4):
             nc.sync.dma_start(
@@ -94,6 +95,7 @@ def tile_extremeoptimizationlayer_pa_w4_kernel(tc, x, W_bytes, W_scale, b, gamma
         x_scales = keep.tile([P, NG, B], U8, name="x_scales", align_bytes=64)
         x_grouped = keep.tile([P, NG, B, T], BF16, name="x_grouped", align_bytes=64)
         vec = keep.tile([P, 3 * UNITS, T], F32, name="vec")
+        gain = keep.tile([P, UNITS, 2, T], F32, name="gain")
 
         def turn_x():
             x_words = x_sb[:].bitcast(F32)
@@ -103,16 +105,15 @@ def tile_extremeoptimizationlayer_pa_w4_kernel(tc, x, W_bytes, W_scale, b, gamma
                     for u in range(2):
                         nc.tensor.transpose(xt[:, r, u, :], x_words[:, r, 256 * g + u : 256 * (g + 1) : 2], ident[:])
                 dst = x_grouped[:, g].bitcast(F32).rearrange("p (r n) u -> p r n u", r=2)
-                nc.scalar.copy(dst, xt[:].rearrange("p r u n -> p r n u"))
+                nc.vector.tensor_copy(dst, xt[:].rearrange("p r u n -> p r n u"))
 
         def turn_vectors():
             vt = hps.tile([P, 2, P], F32, name="h")
             for u in range(2):
                 nc.tensor.transpose(vt[:, u, :], vrows[:].bitcast(F32)[:, u::2], ident[:])
             halves = vt[:].bitcast(BF16).rearrange("p u (r e) -> p r u e", e=2)
-            for v, factor in enumerate((1.0 / B, float(B), 1.0)):
-                rows = slice(UNITS * v, UNITS * (v + 1))
-                nc.scalar.activation(vec[:, rows, :].rearrange("p r (u e) -> p r u e", e=2), halves[:, rows], ACT.Copy, scale=factor)
+            nc.scalar.copy(vec[:].rearrange("p r (u e) -> p r u e", e=2), halves[:, 0 : 3 * UNITS])
+            nc.scalar.copy(gain[:, :, 0, :].rearrange("p r (u e) -> p r u e", e=2), halves[:, UNITS : 2 * UNITS])
 
         def quant_x():
             nc.vector.quantize_mx(
@@ -126,44 +127,52 @@ def tile_extremeoptimizationlayer_pa_w4_kernel(tc, x, W_bytes, W_scale, b, gamma
             for n in range(2):
                 acc[m, n] = accps.tile([P, KP], F32, name="acc%d%d" % (m, n))
 
-        plane, grouped, woven, codes, scales = {}, {}, {}, {}, {}
+        plane, grouped, woven, codes, scales, bn = {}, {}, {}, {}, {}, {}
         h, a, mean, sq, std, scl, off, tmp, nplane, ngrp, act_codes, act_scales = ({} for n in range(12))
 
-        def widen(i, g, rows):
-            if (i, g) not in plane:
-                plane[i, g] = work.tile([P, T, KP], BF16, name="plane%d" % g, align_bytes=64)
-            for j in rows:
+        def widen(i, g):
+            plane[i, g] = work.tile([P, T, KP], BF16, name="plane%d" % g, align_bytes=64)
+            for j in range(T):
                 nc.vector.tensor_scalar(
                     plane[i, g][:, j, :], wbytes[i, g][:, j, :].bitcast(FP8), kscale[:, g * T + j : g * T + j + 1], None, op0=ALU.mult
                 )
 
-        def group_tile(i, g):
-            if (i, g) not in grouped:
-                grouped[i, g] = work.tile([P, T, P, T], BF16, name="grouped%d" % g, align_bytes=64)
-            return grouped[i, g]
+        def widen_pairs(i, g):
+            plane[i, g] = work.tile([P, 2, KP, 2], BF16, name="plane%d" % g, align_bytes=64)
+            for j in (0, 2, 1, 3):
+                nc.vector.tensor_scalar(
+                    plane[i, g][:, j // 2, :, j % 2], wbytes[i, g][:, j, :].bitcast(FP8), kscale[:, g * T + j : g * T + j + 1], None, op0=ALU.mult
+                )
 
-        def lay_out(copy, i, g, m0, m1):
-            dst = group_tile(i, g)[:, :, m0:m1, :].rearrange("p t (q e) j -> p q t j e", e=2)
-            src = plane[i, g][:, :, T * m0 : T * m1].rearrange("p j (q e t) -> p q t j e", e=2, t=T)
+        def lay_out(i, g):
+            grouped[i, g] = work.tile([P, T, P, T], BF16, name="grouped%d" % g, align_bytes=64)
+            dst = grouped[i, g][:].rearrange("p t (q e) j -> p q t j e", e=2)
+            src = plane[i, g][:].rearrange("p j (q e t) -> p q t j e", e=2, t=T)
+            nc.scalar.copy(dst, src)
+
+        def merge(i, g, copy=nc.scalar.copy):
+            grouped[i, g] = work.tile([P, T, P, T], BF16, name="grouped%d" % g, align_bytes=64)
+            dst = grouped[i, g][:].bitcast(F32).rearrange("p t m u -> p m t u")
+            src = plane[i, g][:].bitcast(F32).rearrange("p u (m t) z -> p m t (u z)", t=T)
             copy(dst, src)
 
         def weave(i):
-            for bank, cuts in enumerate(WOVEN):
-                quads = cuts[-1] - cuts[0]
-                woven[i, bank] = wps.tile([P, T, quads, T], BF16, name="woven")
-                for m0, m1 in zip(cuts[:-1], cuts[1:]):
+            for bank in range(2):
+                woven[i, bank] = wps.tile([P, T, P // 2, T], BF16, name="woven")
+                for part in range(2):
+                    c0 = P * (2 * bank + part)
                     nc.tensor.matmul(
-                        woven[i, bank][:, :, m0 - cuts[0] : m1 - cuts[0], :].rearrange("p t m j -> p m t j"),
+                        woven[i, bank][:, :, 32 * part : 32 * part + 32, :].rearrange("p t m j -> p m t j"),
                         lhsT=ident16[:],
-                        rhs=plane[i, 1][:, :, T * m0 : T * m1].rearrange("p j (m t) -> p m t j", t=T),
+                        rhs=plane[i, 1][:, :, c0 : c0 + P].rearrange("p j (m t) -> p m t j", t=T),
                         start=True,
                         stop=True,
                     )
 
         def unweave(i):
-            for bank, cuts in enumerate(WOVEN):
-                nc.scalar.copy(group_tile(i, 1)[:, :, cuts[0] : cuts[-1], :], woven[i, bank][:])
-            lay_out(nc.scalar.copy, i, 1, WOVEN[-1][-1], P)
+            grouped[i, 1] = work.tile([P, T, P, T], BF16, name="grouped1", align_bytes=64)
+            for bank in range(2):
+                nc.scalar.copy(grouped[i, 1][:, :, 64 * bank : 64 * bank + 64, :], woven[i, bank][:])
 
         def quant(i, g):
             codes[i, g] = work.tile([P, KP], U32, name="codes%d" % g, align_bytes=64)
@@ -175,24 +184,24 @@ def tile_extremeoptimizationlayer_pa_w4_kernel(tc, x, W_bytes, W_scale, b, gamma
                 h[i, half] = hps.tile([P, 2, B], F32, name="h")
                 for s in range(2):
                     c = slice(P * (2 * half + s), P * (2 * half + s + 1))
-                    for g in range(NG):
+                    for g in (1, 0):
                         nc.tensor.matmul_mx(
                             h[i, half][:, s, :],
                             lhsT=codes[i, g][:, c].bitcast(FP8X4),
                             lhsT_scale=scales[i, g][:, c],
                             rhs=x_codes[:, g, :].bitcast(FP8X4),
                             rhs_scale=x_scales[:, g, :],
-                            start=(g == 0),
-                            stop=(g == NG - 1),
+                            start=(g == 1),
+                            stop=(g == 0),
                         )
 
-        def relu(i):
-            a[i] = deep.tile([P, T, B], F32, name="a")
-            mean[i] = deep.tile([P, T], F32, name="mean")
-            for t in range(T):
-                nc.scalar.activation(
-                    a[i][:, t, :], h[i, t // 2][:, t % 2, :], ACT.Relu, bias=vec[:, i, t : t + 1], scale=1.0 / B, accum_out=mean[i][:, t : t + 1]
-                )
+        def relu(i, rows=range(T)):
+            if i not in a:
+                a[i] = deep.tile([P, T, B], F32, name="a")
+                mean[i] = deep.tile([P, T], F32, name="mean")
+            for t in rows:
+                total = None if i == LAST else mean[i][:, t : t + 1]
+                nc.scalar.activation(a[i][:, t, :], h[i, t // 2][:, t % 2, :], ACT.Relu, bias=vec[:, i, t : t + 1], accum_out=total)
 
         def square(i):
             sq[i] = work.tile([P, T], F32, name="sq")
@@ -202,40 +211,52 @@ def tile_extremeoptimizationlayer_pa_w4_kernel(tc, x, W_bytes, W_scale, b, gamma
                     junk[:, t, :], a[i][:, t, :], ACT.Square, bias=mean[i][:, t : t + 1], scale=-float(B), accum_out=sq[i][:, t : t + 1]
                 )
 
+        def moments(i, half):
+            if half == 0:
+                bn[i] = work.tile([P, T, 3], F32, name="bn")
+            pair = a[i][:, 2 * half : 2 * half + 2, :].rearrange("p t n -> p n t")
+            nc.vector.bn_stats(bn[i][:, 2 * half : 2 * half + 2, :].rearrange("p t s -> p (t s)"), pair)
+
         def root(i):
-            std[i] = work.tile([P, T], F32, name="std")
-            nc.scalar.activation(std[i][:], sq[i][:], ACT.Sqrt, bias=eps[:], scale=1.0 / B)
+            std[i] = work.tile([P, 1, T], F32, name="std")
+            if i in bn:
+                nc.scalar.activation(std[i][:, 0, :], bn[i][:, :, 2], ACT.Abs_reciprocal_sqrt, bias=eps[:], scale=1.0 / B)
+            else:
+                nc.scalar.activation(std[i][:, 0, :], sq[i][:], ACT.Abs_reciprocal_sqrt, bias=eps[:], scale=1.0 / B**3)
 
-        def coeff(i, stage):
-            if stage == 0:
-                tmp[i] = work.tile([P, T], F32, name="rstd")
-                nc.vector.reciprocal(tmp[i][:], std[i][:])
-            if stage == 1:
-                scl[i] = work.tile([P, T], F32, name="scl")
-                nc.vector.tensor_tensor(scl[i][:], tmp[i][:], vec[:, UNITS + i, :], op=ALU.mult)
-            if stage == 2:
-                tmp[i] = work.tile([P, T], F32, name="shift")
-                nc.vector.scalar_tensor_tensor(tmp[i][:], mean[i][:], -1.0 / B, scl[i][:], op0=ALU.mult, op1=ALU.mult)
-            if stage == 3:
-                off[i] = work.tile([P, T], F32, name="off")
-                nc.vector.tensor_tensor(off[i][:], tmp[i][:], vec[:, 2 * UNITS + i, :], op=ALU.add)
+        def centre(i):
+            if i in bn:
+                nc.vector.scalar_tensor_tensor(gain[:, i, 1, :], bn[i][:, :, 1], -1.0, gain[:, i, 0, :], op0=ALU.mult, op1=ALU.mult)
+            else:
+                nc.vector.scalar_tensor_tensor(gain[:, i, 1, :], mean[i][:], -1.0 / B, gain[:, i, 0, :], op0=ALU.mult, op1=ALU.mult)
 
-        def norm(i):
-            nplane[i] = work.tile([P, T, B], BF16, name="nplane", align_bytes=64)
-            for t in range(T):
-                nc.vector.tensor_scalar(nplane[i][:, t, :], a[i][:, t, :], scl[i][:, t : t + 1], off[i][:, t : t + 1], op0=ALU.mult, op1=ALU.add)
+        def slope(i):
+            scl[i] = work.tile([P, 2, T], F32, name="scl")
+            nc.vector.tensor_tensor(scl[i][:], std[i][:].to_broadcast([P, 2, T]), gain[:, i], op=ALU.mult)
 
-        def nmerge(i):
+        def offset(i):
+            off[i] = work.tile([P, T], F32, name="off")
+            nc.vector.tensor_tensor(off[i][:], scl[i][:, 1, :], vec[:, 2 * UNITS + i, :], op=ALU.add)
+
+        def norm(i, rows=(0, 2, 1, 3)):
+            if i not in nplane:
+                nplane[i] = work.tile([P, 2, B, 2], BF16, name="nplane", align_bytes=64)
+            for t in rows:
+                nc.vector.tensor_scalar(
+                    nplane[i][:, t // 2, :, t % 2], a[i][:, t, :], scl[i][:, 0, t : t + 1], off[i][:, t : t + 1], op0=ALU.mult, op1=ALU.add
+                )
+
+        def nmerge(i, copy):
             ngrp[i] = work.tile([P, B, T], BF16, name="ngrp", align_bytes=64)
-            nc.scalar.copy(ngrp[i][:].rearrange("p (c e) t -> p c t e", e=2), nplane[i][:].rearrange("p t (c e) -> p c t e", e=2))
+            copy(ngrp[i][:].bitcast(F32), nplane[i][:].bitcast(F32).rearrange("p u n z -> p n (u z)"))
 
         def nquant(i):
             act_codes[i] = work.tile([P, B], U32, name="act_codes", align_bytes=64)
             act_scales[i] = work.tile([P, B], U8, name="act_scales", align_bytes=64)
             nc.vector.quantize_mx(act_codes[i][:].bitcast(FP8X4), act_scales[i][:], ngrp[i][:].rearrange("p n t -> p (n t)"))
 
-        def mm2(i):
-            for m in range(2):
+        def mm2(i, halves=(0, 1)):
+            for m in halves:
                 rows = slice(P * m, P * (m + 1))
                 for n in range(2):
                     nc.tensor.matmul_mx(
@@ -249,41 +270,109 @@ def tile_extremeoptimizationlayer_pa_w4_kernel(tc, x, W_bytes, W_scale, b, gamma
                     )
 
         def when(f, i, *args):
-            if 0 <= i < UNITS:
+            if i >= 0:
                 f(i, *args)
 
-        def lay_out_pass0(i):
-            lay_out(nc.scalar.copy if i < 2 else nc.vector.tensor_copy, i, 0, 0, P)
-
-        for s in range(UNITS + 3):
-            when(widen, s, 1, range(T))
-            if s == 0:
-                turn_x()
-                turn_vectors()
+        for s in range(UNITS):
+            if COPIED <= s < PAIRED:
+                widen_pairs(s, 1)
+            else:
+                widen(s, 1)
+            when(relu, s - 2)
+            if s >= PAIRED:
+                weave(s)
+            when(mm2, s - 4)
+            when(norm, s - 3)
             when(square, s - 2)
+            widen_pairs(s, 0)
+            when(nmerge, s - 3, nc.scalar.copy)
             when(root, s - 2)
-            when(weave, s)
-            when(quant, s - 1, 0)
+            if s == 1:
+                turn_x()
             when(quant, s - 1, 1)
-            when(mm1, s - 1)
-            when(nmerge, s - 3)
-            for j in range(T):
-                when(widen, s, 0, (j,))
-                when(coeff, s - 2, j)
-            if s == 0:
+            if s == 1:
                 quant_x()
-            when(unweave, s)
+            when(centre, s - 2)
+            if s < COPIED:
+                lay_out(s, 1)
+            elif s < PAIRED:
+                merge(s, 1)
+            else:
+                unweave(s)
+            if s == 1:
+                turn_vectors()
+            when(quant, s - 1, 0)
+            when(mm1, s - 1)
+            if s == LAST:
+                merge(s, 0, nc.vector.tensor_copy)
+            when(slope, s - 2)
             when(nquant, s - 3)
-            when(mm2, s - 3)
-            when(norm, s - 2)
-            when(relu, s - 1)
-            when(lay_out_pass0, s)
+            when(offset, s - 2)
+            if s < LAST:
+                merge(s, 0)
 
-        for m in range(2):
-            for n in range(2):
-                z = work.tile([P, KP], F32, name="z")
-                cols = slice(KP * n, KP * (n + 1))
-                nc.vector.tensor_tensor(z[:], acc[m, n][:], bf1_b[:, cols], op=ALU.add)
-                o = work.tile([P, KP], F32, name="o")
-                nc.scalar.activation(o[:], z[:], ACT.Relu)
-                nc.sync.dma_start(out=out[P * m : P * (m + 1), cols], in_=o[:])
+        def norm_half(i, m):
+            nplane[i, m] = keep.tile([P, 2, P, 2], BF16, name="nplane_half%d" % m, align_bytes=64)
+            if m == 0:
+                ngrp[i] = work.tile([P, B, T], BF16, name="ngrp", align_bytes=64)
+                act_codes[i] = work.tile([P, B], U32, name="act_codes", align_bytes=64)
+                act_scales[i] = work.tile([P, B], U8, name="act_scales", align_bytes=64)
+            rows = slice(P * m, P * (m + 1))
+            for t in (0, 2, 1, 3):
+                nc.vector.tensor_scalar(
+                    nplane[i, m][:, t // 2, :, t % 2], a[i][:, t, rows], scl[i][:, 0, t : t + 1], off[i][:, t : t + 1], op0=ALU.mult, op1=ALU.add
+                )
+
+        def nmerge_half(i, m, copy):
+            rows = slice(P * m, P * (m + 1))
+            copy(ngrp[i][:, rows].bitcast(F32), nplane[i, m][:].bitcast(F32).rearrange("p u n z -> p n (u z)"))
+
+        def nquant_half(i, m):
+            rows = slice(P * m, P * (m + 1))
+            nc.vector.quantize_mx(act_codes[i][:, rows].bitcast(FP8X4), act_scales[i][:, rows], ngrp[i][:, rows].rearrange("p n t -> p (n t)"))
+
+        quant(LAST, 1)
+        relu(LAST - 1)
+        mm2(LAST - 3)
+        quant(LAST, 0)
+        mm1(LAST)
+        square(LAST - 1)
+        norm(LAST - 2)
+        centre(LAST - 1)
+        nmerge(LAST - 2, nc.vector.tensor_copy)
+        relu(LAST, (0,))
+        root(LAST - 1)
+        relu(LAST, (1, 2, 3))
+        nquant(LAST - 2)
+        mm2(LAST - 2)
+        slope(LAST - 1)
+        moments(LAST, 0)
+        offset(LAST - 1)
+        moments(LAST, 1)
+        root(LAST)
+        norm(LAST - 1, (0, 2))
+        centre(LAST)
+        norm(LAST - 1, (1, 3))
+        nmerge(LAST - 1, nc.scalar.copy)
+        slope(LAST)
+        offset(LAST)
+        norm_half(LAST, 0)
+        nquant(LAST - 1)
+        nmerge_half(LAST, 0, nc.scalar.copy)
+        norm_half(LAST, 1)
+        nmerge_half(LAST, 1, nc.scalar.copy)
+        mm2(LAST - 1, (0,))
+        nquant_half(LAST, 0)
+        mm2(LAST, (0,))
+        mm2(LAST - 1, (1,))
+        nquant_half(LAST, 1)
+        mm2(LAST, (1,))
+
+        pieces = [(0, 0, KP), (0, KP, KP), (1, 0, KP), (1, KP, KP // 2), (1, KP + KP // 2, KP // 2)]
+        for m, c0, width in pieces:
+            cols = slice(c0, c0 + width)
+            z = keep.tile([P, width], F32, name="z%d_%d" % (m, c0))
+            nc.vector.tensor_tensor(z[:], acc[m, c0 // KP][:, c0 % KP : c0 % KP + width], bf1_b[:, cols], op=ALU.add)
+            o = keep.tile([P, width], F32, name="o%d_%d" % (m, c0))
+            nc.scalar.activation(o[:], z[:], ACT.Relu)
+            nc.sync.dma_start(out=out[P * m : P * (m + 1), cols], in_=o[:])

@@ -32,7 +32,8 @@ def tile_extremeoptimizationlayer_pa_w4_kernel(tc, x, W_bytes, W_scale, b, gamma
     with ExitStack() as ctx:
         keep = ctx.enter_context(tc.tile_pool(name="keep", bufs=1))
         work = ctx.enter_context(tc.tile_pool(name="work", bufs=2))
-        deep = ctx.enter_context(tc.tile_pool(name="deep", bufs=3))
+        deep = ctx.enter_context(tc.tile_pool(name="deep", bufs=4))
+        wpool = ctx.enter_context(tc.tile_pool(name="wpool", bufs=4))
         hps = ctx.enter_context(tc.psum_pool(name="hps", bufs=2))
         wps = ctx.enter_context(tc.psum_pool(name="wps", bufs=2))
         accps = ctx.enter_context(tc.psum_pool(name="accps", bufs=1))
@@ -50,10 +51,14 @@ def tile_extremeoptimizationlayer_pa_w4_kernel(tc, x, W_bytes, W_scale, b, gamma
         def load_w(k, g, halves):
             src = W_bytes[k].rearrange("(g p t) o -> g p t o", p=P, t=T)[g]
             cols = slice(KP * halves[0], KP * (halves[-1] + 1))
-            wb = keep.tile([P, T, KP * len(halves)], U8, name="wb%d_%d_%d" % (k, g, halves[0]))
+            if len(halves) == 1:
+                wb = keep.tile([P, T, KP], U8, name="wb_first%d_%d" % (g, halves[0]))
+                wbytes[2 * k + halves[0], g] = wb[:]
+            else:
+                wb = wpool.tile([P, T, DO], U8, name="wb%d" % g)
+                wbytes[2 * k, g] = wb[:]
+                wbytes[2 * k + 1, g] = wb[:, :, KP:DO]
             nc.sync.dma_start(out=wb[:], in_=src[:, :, cols])
-            for n, half in enumerate(halves):
-                wbytes[2 * k + half, g] = wb[:, :, KP * n : KP * (n + 1)]
 
         x_sb = keep.tile([P, 2, DI], BF16, name="x_sb")
         wf = keep.tile([P, UNITS, 2 * DO], U8, name="wf", align_bytes=64)
@@ -65,8 +70,8 @@ def tile_extremeoptimizationlayer_pa_w4_kernel(tc, x, W_bytes, W_scale, b, gamma
         nc.sync.dma_start(out=x_sb[:], in_=x.rearrange("(r p) k -> p r k", p=P))
         load_w(0, 1, (1,))
         load_w(0, 0, (1,))
-        load_w(1, 1, (0, 1))
         load_w(1, 0, (0, 1))
+        load_w(1, 1, (0, 1))
 
         ident = keep.tile([P, P], F32, name="ident")
         make_identity(nc, ident[:])
@@ -83,12 +88,12 @@ def tile_extremeoptimizationlayer_pa_w4_kernel(tc, x, W_bytes, W_scale, b, gamma
                 out=wfs[32 * q : 32 * q + 4].bitcast(I32),
                 in_=Wf1_scales[:, 4 * q : 4 * q + 4, :].rearrange("u q n -> q u n").bitcast(I32),
             )
-        for k in range(2, NB):
-            if k - 2 < 4:
-                u = slice(4 * (k - 2), 4 * (k - 2) + 4)
-                nc.sync.dma_start(out=wf[:, u], in_=Wf1_words[u].rearrange("u p n -> p u n"))
-            load_w(k, 1, (0, 1))
-            load_w(k, 0, (0, 1))
+        for k in range(2, 6):
+            u = slice(4 * (k - 2), 4 * (k - 2) + 4)
+            if k < 5:
+                load_w(k, 0, (0, 1))
+                load_w(k, 1, (0, 1))
+            nc.sync.dma_start(out=wf[:, u], in_=Wf1_words[u].rearrange("u p n -> p u n"))
         nc.sync.dma_start(out=bf1_b[:], in_=bf1.partition_broadcast(P))
 
         x_codes = keep.tile([P, NG, B], U32, name="x_codes", align_bytes=64)
@@ -105,7 +110,7 @@ def tile_extremeoptimizationlayer_pa_w4_kernel(tc, x, W_bytes, W_scale, b, gamma
                     for u in range(2):
                         nc.tensor.transpose(xt[:, r, u, :], x_words[:, r, 256 * g + u : 256 * (g + 1) : 2], ident[:])
                 dst = x_grouped[:, g].bitcast(F32).rearrange("p (r n) u -> p r n u", r=2)
-                nc.vector.tensor_copy(dst, xt[:].rearrange("p r u n -> p r n u"))
+                nc.scalar.copy(dst, xt[:].rearrange("p r u n -> p r n u"))
 
         def turn_vectors():
             vt = hps.tile([P, 2, P], F32, name="h")
@@ -127,33 +132,48 @@ def tile_extremeoptimizationlayer_pa_w4_kernel(tc, x, W_bytes, W_scale, b, gamma
             for n in range(2):
                 acc[m, n] = accps.tile([P, KP], F32, name="acc%d%d" % (m, n))
 
-        plane, grouped, woven, codes, scales, bn = {}, {}, {}, {}, {}, {}
-        h, a, mean, sq, std, scl, off, tmp, nplane, ngrp, act_codes, act_scales = ({} for n in range(12))
+        plane, whole, grouped, woven, codes, scales = ({} for n in range(6))
+        h, a, nplane, ngrp, act_codes, act_scales, pair = ({} for n in range(7))
 
-        def widen(i, g):
-            plane[i, g] = work.tile([P, T, KP], BF16, name="plane%d" % g, align_bytes=64)
-            for j in range(T):
+        def widen(i, g, units, rows=range(T)):
+            if (i, g) not in plane:
+                tile = work.tile([P, T, DO], BF16, name="plane%d" % g, align_bytes=64)
+                for n in range(units):
+                    plane[i + n, g] = tile[:, :, KP * n : KP * (n + 1)]
+                whole[i, g] = tile[:, :, 0 : KP * units]
+            for j in rows:
                 nc.vector.tensor_scalar(
-                    plane[i, g][:, j, :], wbytes[i, g][:, j, :].bitcast(FP8), kscale[:, g * T + j : g * T + j + 1], None, op0=ALU.mult
+                    whole[i, g][:, j, :], wbytes[i, g][:, j, 0 : KP * units].bitcast(FP8), kscale[:, g * T + j : g * T + j + 1], None, op0=ALU.mult
                 )
 
-        def widen_pairs(i, g):
-            plane[i, g] = work.tile([P, 2, KP, 2], BF16, name="plane%d" % g, align_bytes=64)
-            for j in (0, 2, 1, 3):
+        def widen_pairs(i, g, units, rows=(0, 2, 1, 3)):
+            if (i, g) not in plane:
+                tile = work.tile([P, 2, DO, 2], BF16, name="plane%d" % g, align_bytes=64)
+                for n in range(units):
+                    plane[i + n, g] = tile[:, :, KP * n : KP * (n + 1), :]
+                whole[i, g] = tile[:, :, 0 : KP * units, :]
+            for j in rows:
                 nc.vector.tensor_scalar(
-                    plane[i, g][:, j // 2, :, j % 2], wbytes[i, g][:, j, :].bitcast(FP8), kscale[:, g * T + j : g * T + j + 1], None, op0=ALU.mult
+                    whole[i, g][:, j // 2, :, j % 2],
+                    wbytes[i, g][:, j, 0 : KP * units].bitcast(FP8),
+                    kscale[:, g * T + j : g * T + j + 1],
+                    None,
+                    op0=ALU.mult,
                 )
+
+        def group_tile(i, g):
+            if i not in grouped:
+                grouped[i] = work.tile([P, NG, T, P, T], BF16, name="grouped", align_bytes=64)
+            return grouped[i][:, g]
 
         def lay_out(i, g):
-            grouped[i, g] = work.tile([P, T, P, T], BF16, name="grouped%d" % g, align_bytes=64)
-            dst = grouped[i, g][:].rearrange("p t (q e) j -> p q t j e", e=2)
-            src = plane[i, g][:].rearrange("p j (q e t) -> p q t j e", e=2, t=T)
+            dst = group_tile(i, g).rearrange("p t (q e) j -> p q t j e", e=2)
+            src = plane[i, g].rearrange("p j (q e t) -> p q t j e", e=2, t=T)
             nc.scalar.copy(dst, src)
 
         def merge(i, g, copy=nc.scalar.copy):
-            grouped[i, g] = work.tile([P, T, P, T], BF16, name="grouped%d" % g, align_bytes=64)
-            dst = grouped[i, g][:].bitcast(F32).rearrange("p t m u -> p m t u")
-            src = plane[i, g][:].bitcast(F32).rearrange("p u (m t) z -> p m t (u z)", t=T)
+            dst = group_tile(i, g).bitcast(F32).rearrange("p t m u -> p m t u")
+            src = plane[i, g].bitcast(F32).rearrange("p u (m t) z -> p m t (u z)", t=T)
             copy(dst, src)
 
         def weave(i):
@@ -169,15 +189,20 @@ def tile_extremeoptimizationlayer_pa_w4_kernel(tc, x, W_bytes, W_scale, b, gamma
                         stop=True,
                     )
 
-        def unweave(i):
-            grouped[i, 1] = work.tile([P, T, P, T], BF16, name="grouped1", align_bytes=64)
-            for bank in range(2):
-                nc.scalar.copy(grouped[i, 1][:, :, 64 * bank : 64 * bank + 64, :], woven[i, bank][:])
+        def unweave(i, banks=range(2)):
+            for bank in banks:
+                nc.scalar.copy(group_tile(i, 1)[:, :, 64 * bank : 64 * bank + 64, :], woven[i, bank][:])
 
-        def quant(i, g):
-            codes[i, g] = work.tile([P, KP], U32, name="codes%d" % g, align_bytes=64)
-            scales[i, g] = work.tile([P, KP], U8, name="scales%d" % g, align_bytes=64)
-            nc.vector.quantize_mx(codes[i, g][:].bitcast(FP8X4), scales[i, g][:], grouped[i, g][:].rearrange("p t m j -> p (t m j)"))
+        def quant(i, passes=range(NG)):
+            if i not in codes:
+                codes[i] = work.tile([P, NG, KP], U32, name="codes", align_bytes=64)
+                scales[i] = work.tile([P, NG, KP], U8, name="scales", align_bytes=64)
+            g = slice(passes[0], passes[-1] + 1)
+            nc.vector.quantize_mx(
+                codes[i][:, g].rearrange("p g c -> p (g c)").bitcast(FP8X4),
+                scales[i][:, g].rearrange("p g c -> p (g c)"),
+                grouped[i][:, g].rearrange("p g t m j -> p (g t m j)"),
+            )
 
         def mm1(i):
             for half in range(2):
@@ -187,73 +212,81 @@ def tile_extremeoptimizationlayer_pa_w4_kernel(tc, x, W_bytes, W_scale, b, gamma
                     for g in (1, 0):
                         nc.tensor.matmul_mx(
                             h[i, half][:, s, :],
-                            lhsT=codes[i, g][:, c].bitcast(FP8X4),
-                            lhsT_scale=scales[i, g][:, c],
+                            lhsT=codes[i][:, g, c].bitcast(FP8X4),
+                            lhsT_scale=scales[i][:, g, c],
                             rhs=x_codes[:, g, :].bitcast(FP8X4),
                             rhs_scale=x_scales[:, g, :],
                             start=(g == 1),
                             stop=(g == 0),
                         )
 
+        sums = keep.tile([P, UNITS, T], F32, name="sums")
+        squares = keep.tile([P, UNITS, T], F32, name="squares")
+        rstd = keep.tile([P, UNITS, 1, T], F32, name="rstd")
+        slopes = keep.tile([P, UNITS, 2, T], F32, name="slopes")
+        offsets = keep.tile([P, UNITS, T], F32, name="offsets")
+
         def relu(i, rows=range(T)):
             if i not in a:
                 a[i] = deep.tile([P, T, B], F32, name="a")
-                mean[i] = deep.tile([P, T], F32, name="mean")
             for t in rows:
-                total = None if i == LAST else mean[i][:, t : t + 1]
-                nc.scalar.activation(a[i][:, t, :], h[i, t // 2][:, t % 2, :], ACT.Relu, bias=vec[:, i, t : t + 1], accum_out=total)
+                nc.scalar.activation(a[i][:, t, :], h[i, t // 2][:, t % 2, :], ACT.Relu, bias=vec[:, i, t : t + 1], accum_out=sums[:, i, t : t + 1])
 
         def square(i):
-            sq[i] = work.tile([P, T], F32, name="sq")
             junk = work.tile([P, T, B], BF16, name="junk")
             for t in range(T):
                 nc.scalar.activation(
-                    junk[:, t, :], a[i][:, t, :], ACT.Square, bias=mean[i][:, t : t + 1], scale=-float(B), accum_out=sq[i][:, t : t + 1]
+                    junk[:, t, :], a[i][:, t, :], ACT.Square, bias=sums[:, i, t : t + 1], scale=-float(B), accum_out=squares[:, i, t : t + 1]
                 )
 
-        def moments(i, half):
-            if half == 0:
-                bn[i] = work.tile([P, T, 3], F32, name="bn")
-            pair = a[i][:, 2 * half : 2 * half + 2, :].rearrange("p t n -> p n t")
-            nc.vector.bn_stats(bn[i][:, 2 * half : 2 * half + 2, :].rearrange("p t s -> p (t s)"), pair)
+        def root(i, units):
+            u = slice(i, i + units)
+            nc.scalar.activation(rstd[:, u, 0, :], squares[:, u], ACT.Abs_reciprocal_sqrt, bias=eps[:], scale=1.0 / B**3)
 
-        def root(i):
-            std[i] = work.tile([P, 1, T], F32, name="std")
-            if i in bn:
-                nc.scalar.activation(std[i][:, 0, :], bn[i][:, :, 2], ACT.Abs_reciprocal_sqrt, bias=eps[:], scale=1.0 / B)
-            else:
-                nc.scalar.activation(std[i][:, 0, :], sq[i][:], ACT.Abs_reciprocal_sqrt, bias=eps[:], scale=1.0 / B**3)
+        def centre(i, units):
+            u = slice(i, i + units)
+            nc.vector.scalar_tensor_tensor(gain[:, u, 1, :], sums[:, u], -1.0 / B, gain[:, u, 0, :], op0=ALU.mult, op1=ALU.mult)
 
-        def centre(i):
-            if i in bn:
-                nc.vector.scalar_tensor_tensor(gain[:, i, 1, :], bn[i][:, :, 1], -1.0, gain[:, i, 0, :], op0=ALU.mult, op1=ALU.mult)
-            else:
-                nc.vector.scalar_tensor_tensor(gain[:, i, 1, :], mean[i][:], -1.0 / B, gain[:, i, 0, :], op0=ALU.mult, op1=ALU.mult)
+        def slope(i, units):
+            u = slice(i, i + units)
+            nc.vector.tensor_tensor(slopes[:, u], rstd[:, u].to_broadcast([P, units, 2, T]), gain[:, u], op=ALU.mult)
 
-        def slope(i):
-            scl[i] = work.tile([P, 2, T], F32, name="scl")
-            nc.vector.tensor_tensor(scl[i][:], std[i][:].to_broadcast([P, 2, T]), gain[:, i], op=ALU.mult)
-
-        def offset(i):
-            off[i] = work.tile([P, T], F32, name="off")
-            nc.vector.tensor_tensor(off[i][:], scl[i][:, 1, :], vec[:, 2 * UNITS + i, :], op=ALU.add)
+        def offset(i, units):
+            u = slice(i, i + units)
+            nc.vector.tensor_tensor(offsets[:, u], slopes[:, u, 1, :], vec[:, 2 * UNITS + i : 2 * UNITS + i + units, :], op=ALU.add)
 
         def norm(i, rows=(0, 2, 1, 3)):
             if i not in nplane:
                 nplane[i] = work.tile([P, 2, B, 2], BF16, name="nplane", align_bytes=64)
             for t in rows:
                 nc.vector.tensor_scalar(
-                    nplane[i][:, t // 2, :, t % 2], a[i][:, t, :], scl[i][:, 0, t : t + 1], off[i][:, t : t + 1], op0=ALU.mult, op1=ALU.add
+                    nplane[i][:, t // 2, :, t % 2], a[i][:, t, :], slopes[:, i, 0, t : t + 1], offsets[:, i, t : t + 1], op0=ALU.mult, op1=ALU.add
                 )
 
+        def pair_tiles(i):
+            first = i - i % 2
+            if first not in ngrp:
+                tiles = (
+                    work.tile([P, 2, B, T], BF16, name="ngrp", align_bytes=64),
+                    work.tile([P, 2, B], U32, name="act_codes", align_bytes=64),
+                    work.tile([P, 2, B], U8, name="act_scales", align_bytes=64),
+                )
+                for n in range(2):
+                    ngrp[first + n], act_codes[first + n], act_scales[first + n] = (tile[:, n] for tile in tiles)
+                pair[first] = tiles
+
         def nmerge(i, copy):
-            ngrp[i] = work.tile([P, B, T], BF16, name="ngrp", align_bytes=64)
-            copy(ngrp[i][:].bitcast(F32), nplane[i][:].bitcast(F32).rearrange("p u n z -> p n (u z)"))
+            pair_tiles(i)
+            copy(ngrp[i].bitcast(F32), nplane[i][:].bitcast(F32).rearrange("p u n z -> p n (u z)"))
 
         def nquant(i):
-            act_codes[i] = work.tile([P, B], U32, name="act_codes", align_bytes=64)
-            act_scales[i] = work.tile([P, B], U8, name="act_scales", align_bytes=64)
-            nc.vector.quantize_mx(act_codes[i][:].bitcast(FP8X4), act_scales[i][:], ngrp[i][:].rearrange("p n t -> p (n t)"))
+            nc.vector.quantize_mx(act_codes[i].bitcast(FP8X4), act_scales[i], ngrp[i].rearrange("p n t -> p (n t)"))
+
+        def nquant_pair(i):
+            values, words, bytes_ = pair[i]
+            nc.vector.quantize_mx(
+                words[:].rearrange("p u n -> p (u n)").bitcast(FP8X4), bytes_[:].rearrange("p u n -> p (u n)"), values[:].rearrange("p u n t -> p (u n t)")
+            )
 
         def mm2(i, halves=(0, 1)):
             for m in halves:
@@ -273,54 +306,84 @@ def tile_extremeoptimizationlayer_pa_w4_kernel(tc, x, W_bytes, W_scale, b, gamma
             if i >= 0:
                 f(i, *args)
 
-        for s in range(UNITS):
-            if COPIED <= s < PAIRED:
-                widen_pairs(s, 1)
-            else:
-                widen(s, 1)
-            when(relu, s - 2)
-            if s >= PAIRED:
-                weave(s)
-            when(mm2, s - 4)
-            when(norm, s - 3)
-            when(square, s - 2)
-            widen_pairs(s, 0)
-            when(nmerge, s - 3, nc.scalar.copy)
-            when(root, s - 2)
-            if s == 1:
-                turn_x()
-            when(quant, s - 1, 1)
-            if s == 1:
-                quant_x()
-            when(centre, s - 2)
-            if s < COPIED:
-                lay_out(s, 1)
-            elif s < PAIRED:
+        def lay_out_pass1(s):
+            if s < PAIRED:
                 merge(s, 1)
             else:
                 unweave(s)
-            if s == 1:
-                turn_vectors()
-            when(quant, s - 1, 0)
-            when(mm1, s - 1)
-            if s == LAST:
-                merge(s, 0, nc.vector.tensor_copy)
-            when(slope, s - 2)
-            when(nquant, s - 3)
-            when(offset, s - 2)
-            if s < LAST:
-                merge(s, 0)
+
+        widen(0, 1, 1)
+        lay_out(0, 1)
+        widen_pairs(0, 0, 1)
+        merge(0, 0)
+        widen(1, 1, 1)
+        turn_x()
+        widen_pairs(1, 0, 1)
+        lay_out(1, 1)
+        turn_vectors()
+        quant_x()
+        quant(0)
+        mm1(0)
+        merge(1, 0)
+        widen_pairs(2, 0, 2)
+
+        for s in range(2, UNITS - 2, 2):
+            if s < PAIRED:
+                widen_pairs(s, 1, 1)
+            else:
+                widen(s, 1, 2)
+            relu(s - 2)
+            when(mm2, s - 6)
+            if s >= PAIRED:
+                weave(s)
+            when(norm, s - 4)
+            square(s - 2)
+            quant(s - 1)
+            mm1(s - 1)
+            lay_out_pass1(s)
+            if s >= 4:
+                norm(s - 3)
+            merge(s, 0)
+            when(nmerge, s - 4, nc.scalar.copy)
+            if 5 <= s // 2 + 3 < NB:
+                load_w(s // 2 + 3, 0, (0, 1))
+                load_w(s // 2 + 3, 1, (0, 1))
+            o = s + 1
+            relu(o - 2)
+            if o >= PAIRED:
+                weave(o)
+            else:
+                widen_pairs(o, 1, 1)
+            if s >= 6:
+                mm2(s - 5)
+            widen_pairs(o + 1, 0, 2, (0, 2))
+            square(o - 2)
+            if s >= 4:
+                nmerge(s - 3, nc.vector.tensor_copy)
+            quant(o - 1)
+            mm1(o - 1)
+            centre(s - 2, 2)
+            widen_pairs(o + 1, 0, 2, (1,))
+            if o < PAIRED:
+                merge(o, 1)
+                root(s - 2, 2)
+            else:
+                unweave(o, (0,))
+                root(s - 2, 2)
+                unweave(o, (1,))
+            widen_pairs(o + 1, 0, 2, (3,))
+            slope(s - 2, 2)
+            when(nquant_pair, s - 4)
+            offset(s - 2, 2)
+            merge(o, 0)
 
         def norm_half(i, m):
+            pair_tiles(i)
             nplane[i, m] = keep.tile([P, 2, P, 2], BF16, name="nplane_half%d" % m, align_bytes=64)
-            if m == 0:
-                ngrp[i] = work.tile([P, B, T], BF16, name="ngrp", align_bytes=64)
-                act_codes[i] = work.tile([P, B], U32, name="act_codes", align_bytes=64)
-                act_scales[i] = work.tile([P, B], U8, name="act_scales", align_bytes=64)
             rows = slice(P * m, P * (m + 1))
             for t in (0, 2, 1, 3):
                 nc.vector.tensor_scalar(
-                    nplane[i, m][:, t // 2, :, t % 2], a[i][:, t, rows], scl[i][:, 0, t : t + 1], off[i][:, t : t + 1], op0=ALU.mult, op1=ALU.add
+                    nplane[i, m][:, t // 2, :, t % 2], a[i][:, t, rows], slopes[:, i, 0, t : t + 1], offsets[:, i, t : t + 1], op0=ALU.mult, op1=ALU.add
                 )
 
         def nmerge_half(i, m, copy):
@@ -331,40 +394,69 @@ def tile_extremeoptimizationlayer_pa_w4_kernel(tc, x, W_bytes, W_scale, b, gamma
             rows = slice(P * m, P * (m + 1))
             nc.vector.quantize_mx(act_codes[i][:, rows].bitcast(FP8X4), act_scales[i][:, rows], ngrp[i][:, rows].rearrange("p n t -> p (n t)"))
 
-        quant(LAST, 1)
-        relu(LAST - 1)
-        mm2(LAST - 3)
-        quant(LAST, 0)
-        mm1(LAST)
-        square(LAST - 1)
-        norm(LAST - 2)
-        centre(LAST - 1)
-        nmerge(LAST - 2, nc.vector.tensor_copy)
-        relu(LAST, (0,))
-        root(LAST - 1)
-        relu(LAST, (1, 2, 3))
-        nquant(LAST - 2)
-        mm2(LAST - 2)
-        slope(LAST - 1)
-        moments(LAST, 0)
-        offset(LAST - 1)
-        moments(LAST, 1)
-        root(LAST)
-        norm(LAST - 1, (0, 2))
-        centre(LAST)
-        norm(LAST - 1, (1, 3))
-        nmerge(LAST - 1, nc.scalar.copy)
-        slope(LAST)
-        offset(LAST)
+        widen(14, 1, 2)
+        relu(12)
+        mm2(8)
+        weave(14)
+        merge(14, 0, nc.vector.tensor_copy)
+        square(12)
+        quant(13)
+        mm1(13)
+        unweave(14)
+        weave(15)
+        mm2(9)
+        merge(15, 0, nc.vector.tensor_copy)
+        norm(10)
+        relu(13)
+        quant(14)
+        mm1(14)
+        unweave(15)
+        norm(11)
+        nmerge(10, nc.vector.tensor_copy)
+        square(13)
+        quant(15)
+        nmerge(11, nc.vector.tensor_copy)
+        centre(12, 2)
+        relu(14, (0,))
+        root(12, 2)
+        relu(14, (1, 2, 3))
+        mm1(15)
+        nquant_pair(10)
+        mm2(10)
+        mm2(11)
+        slope(12, 2)
+        square(14)
+        offset(12, 2)
+        centre(14, 1)
+        norm(12)
+        relu(15, (0,))
+        root(14, 1)
+        relu(15, (1, 2, 3))
+        norm(13)
+        nmerge(12, nc.vector.tensor_copy)
+        square(15)
+        slope(14, 1)
+        nmerge(13, nc.vector.tensor_copy)
+        offset(14, 1)
+        nquant(12)
+        mm2(12)
+        centre(LAST, 1)
+        nquant(13)
+        mm2(13)
+        norm(14)
+        root(LAST, 1)
+        nmerge(14, nc.scalar.copy)
+        slope(LAST, 1)
+        offset(LAST, 1)
         norm_half(LAST, 0)
-        nquant(LAST - 1)
+        nquant(14)
         nmerge_half(LAST, 0, nc.scalar.copy)
         norm_half(LAST, 1)
         nmerge_half(LAST, 1, nc.scalar.copy)
-        mm2(LAST - 1, (0,))
+        mm2(14, (0,))
         nquant_half(LAST, 0)
         mm2(LAST, (0,))
-        mm2(LAST - 1, (1,))
+        mm2(14, (1,))
         nquant_half(LAST, 1)
         mm2(LAST, (1,))
 

@@ -22,7 +22,7 @@ NG = DI // KP
 UNITS = NB * DO // KP
 LAST = UNITS - 1
 EPS = 1e-5
-COPIED, PAIRED = 2, 4
+COPIED, PAIRED = 2, 2
 
 FLOPS = 2 * B * DI * NB * DO + 2 * B * NB * DO * DO
 
@@ -179,12 +179,13 @@ def tile_extremeoptimizationlayer_pa_w4_kernel(tc, x, W_bytes, W_scale, b, gamma
         def weave(i):
             for bank in range(2):
                 woven[i, bank] = wps.tile([P, T, P // 2, T], BF16, name="woven")
-                for part in range(2):
-                    c0 = P * (2 * bank + part)
+            for u in range(2):
+                for bank in range(2):
+                    channels = plane[i, 1][:, 2 * u : 2 * u + 2, 2 * P * bank : 2 * P * (bank + 1)]
                     nc.tensor.matmul(
-                        woven[i, bank][:, :, 32 * part : 32 * part + 32, :].rearrange("p t m j -> p m t j"),
+                        woven[i, bank][:, :, :, 2 * u : 2 * u + 2].rearrange("p t m e -> p m t e"),
                         lhsT=ident16[:],
-                        rhs=plane[i, 1][:, :, c0 : c0 + P].rearrange("p j (m t) -> p m t j", t=T),
+                        rhs=channels.rearrange("p e (m t) -> p m t e", t=T),
                         start=True,
                         stop=True,
                     )
@@ -333,18 +334,18 @@ def tile_extremeoptimizationlayer_pa_w4_kernel(tc, x, W_bytes, W_scale, b, gamma
             else:
                 widen(s, 1, 2)
             relu(s - 2)
-            when(mm2, s - 6)
             if s >= PAIRED:
                 weave(s)
             when(norm, s - 4)
             square(s - 2)
             quant(s - 1)
             mm1(s - 1)
-            lay_out_pass1(s)
+            when(mm2, s - 6)
+            merge(s, 0)
             if s >= 4:
                 norm(s - 3)
-            merge(s, 0)
             when(nmerge, s - 4, nc.scalar.copy)
+            lay_out_pass1(s)
             if 5 <= s // 2 + 3 < NB:
                 load_w(s // 2 + 3, 0, (0, 1))
                 load_w(s // 2 + 3, 1, (0, 1))
@@ -354,28 +355,23 @@ def tile_extremeoptimizationlayer_pa_w4_kernel(tc, x, W_bytes, W_scale, b, gamma
                 weave(o)
             else:
                 widen_pairs(o, 1, 1)
-            if s >= 6:
-                mm2(s - 5)
             widen_pairs(o + 1, 0, 2, (0, 2))
             square(o - 2)
             if s >= 4:
                 nmerge(s - 3, nc.vector.tensor_copy)
             quant(o - 1)
             mm1(o - 1)
+            if s >= 6:
+                mm2(s - 5)
             centre(s - 2, 2)
             widen_pairs(o + 1, 0, 2, (1,))
-            if o < PAIRED:
-                merge(o, 1)
-                root(s - 2, 2)
-            else:
-                unweave(o, (0,))
-                root(s - 2, 2)
-                unweave(o, (1,))
+            merge(o, 0)
+            root(s - 2, 2)
             widen_pairs(o + 1, 0, 2, (3,))
             slope(s - 2, 2)
             when(nquant_pair, s - 4)
             offset(s - 2, 2)
-            merge(o, 0)
+            lay_out_pass1(o)
 
         def norm_half(i, m):
             pair_tiles(i)
@@ -394,23 +390,22 @@ def tile_extremeoptimizationlayer_pa_w4_kernel(tc, x, W_bytes, W_scale, b, gamma
             rows = slice(P * m, P * (m + 1))
             nc.vector.quantize_mx(act_codes[i][:, rows].bitcast(FP8X4), act_scales[i][:, rows], ngrp[i][:, rows].rearrange("p n t -> p (n t)"))
 
-        widen(14, 1, 2)
+        widen_pairs(14, 1, 2, (0, 2))
         relu(12)
-        mm2(8)
-        weave(14)
-        merge(14, 0, nc.vector.tensor_copy)
-        square(12)
         quant(13)
         mm1(13)
-        unweave(14)
-        weave(15)
+        mm2(8)
         mm2(9)
-        merge(15, 0, nc.vector.tensor_copy)
+        widen_pairs(14, 1, 2, (1, 3))
+        square(12)
+        merge(14, 0)
         norm(10)
+        merge(14, 1, nc.vector.tensor_copy)
         relu(13)
         quant(14)
         mm1(14)
-        unweave(15)
+        merge(15, 0)
+        merge(15, 1)
         norm(11)
         nmerge(10, nc.vector.tensor_copy)
         square(13)

@@ -178,21 +178,16 @@ def tile_extremeoptimizationlayer_pa_w4_kernel(tc, x, W_bytes, W_scale, b, gamma
 
         def weave(i):
             for bank in range(2):
-                woven[i, bank] = wps.tile([P, T, P // 2, T], BF16, name="woven")
+                woven[i, bank] = wps.tile([P, 2, 2 * P, 2], BF16, name="woven")
             for u in range(2):
                 for bank in range(2):
                     channels = plane[i, 1][:, 2 * u : 2 * u + 2, 2 * P * bank : 2 * P * (bank + 1)]
-                    nc.tensor.matmul(
-                        woven[i, bank][:, :, :, 2 * u : 2 * u + 2].rearrange("p t m e -> p m t e"),
-                        lhsT=ident16[:],
-                        rhs=channels.rearrange("p e (m t) -> p m t e", t=T),
-                        start=True,
-                        stop=True,
-                    )
+                    nc.tensor.matmul(woven[i, bank][:, u], lhsT=ident16[:], rhs=channels.rearrange("p e c -> p c e"), start=True, stop=True)
 
-        def unweave(i, banks=range(2)):
-            for bank in banks:
-                nc.scalar.copy(group_tile(i, 1)[:, :, 64 * bank : 64 * bank + 64, :], woven[i, bank][:])
+        def unweave(i):
+            for bank in range(2):
+                dst = group_tile(i, 1)[:, :, 64 * bank : 64 * bank + 64, :].bitcast(F32).rearrange("p t m u -> p m t u")
+                nc.scalar.copy(dst, woven[i, bank][:].bitcast(F32).rearrange("p u (m t) z -> p m t (u z)", t=T))
 
         def quant(i, passes=range(NG)):
             if i not in codes:

@@ -186,8 +186,8 @@ def tile_extremeoptimizationlayer_pa_w4_kernel(tc, x, W_bytes, W_scale, b, gamma
 
         def unweave(i):
             for bank in range(2):
-                dst = group_tile(i, 1)[:, :, 64 * bank : 64 * bank + 64, :].bitcast(F32).rearrange("p t m u -> p m t u")
-                nc.scalar.copy(dst, woven[i, bank][:].bitcast(F32).rearrange("p u (m t) z -> p m t (u z)", t=T))
+                dst = group_tile(i, 1)[:, :, 64 * bank : 64 * bank + 64, :].bitcast(F32)
+                nc.scalar.copy(dst, woven[i, bank][:].bitcast(F32).rearrange("p u (m t) z -> p t m (u z)", t=T))
 
         def quant(i, passes=range(NG)):
             if i not in codes:

@@ -182,7 +182,13 @@ def tile_extremeoptimizationlayer_pa_w4_kernel(tc, x, W_bytes, W_scale, b, gamma
             for u in range(2):
                 for bank in range(2):
                     channels = plane[i, 1][:, 2 * u : 2 * u + 2, 2 * P * bank : 2 * P * (bank + 1)]
-                    nc.tensor.matmul(woven[i, bank][:, u], lhsT=ident16[:], rhs=channels.rearrange("p e c -> p c e"), start=True, stop=True)
+                    nc.tensor.matmul(
+                        woven[i, bank][:, u].rearrange("p (q c) e -> p q e c", c=8),
+                        lhsT=ident16[:],
+                        rhs=channels.rearrange("p e (q c) -> p q e c", c=8),
+                        start=True,
+                        stop=True,
+                    )
 
         def unweave(i):
             for bank in range(2):

@@ -22,56 +22,64 @@ NG = DI // KP
 UNITS = NB * DO // KP
 LAST = UNITS - 1
 EPS = 1e-5
-COPIED, PAIRED = 2, 2
+BANK_QUADS = 64
+SPARE_QUADS = 48
+LINE = 8
+W_BUFS = 4
+EVEN_ROWS, ODD_ROWS = (0, 2), (1, 3)
 
 FLOPS = 2 * B * DI * NB * DO + 2 * B * NB * DO * DO
 
 
 def tile_extremeoptimizationlayer_pa_w4_kernel(tc, x, W_bytes, W_scale, b, gamma, beta, Wf1_words, Wf1_scales, bf1, out):
     nc = tc.nc
+    on_scalar, on_vector = nc.scalar.copy, nc.vector.tensor_copy
     with ExitStack() as ctx:
         keep = ctx.enter_context(tc.tile_pool(name="keep", bufs=1))
         work = ctx.enter_context(tc.tile_pool(name="work", bufs=2))
-        deep = ctx.enter_context(tc.tile_pool(name="deep", bufs=4))
-        wpool = ctx.enter_context(tc.tile_pool(name="wpool", bufs=4))
+        apool = ctx.enter_context(tc.tile_pool(name="apool", bufs=4))
+        wpool = ctx.enter_context(tc.tile_pool(name="wpool", bufs=W_BUFS))
         hps = ctx.enter_context(tc.psum_pool(name="hps", bufs=2))
         wps = ctx.enter_context(tc.psum_pool(name="wps", bufs=2))
         accps = ctx.enter_context(tc.psum_pool(name="accps", bufs=1))
         ctx.enter_context(tc.manual_schedule())
 
         kscale = keep.tile([P, NG * T], F32, name="kscale")
-        nc.scalar.dma_start(out=kscale[:].rearrange("p (g t) -> p g t", g=NG), in_=W_scale.rearrange("o (g p t) z -> p (o g) (t z)", p=P, t=T))
+        nc.scalar.dma_start(out=kscale[:].rearrange("p (g j) -> p g j", g=NG), in_=W_scale.rearrange("o (g p j) z -> p (o g) (j z)", p=P, j=T))
         vrows = keep.tile([P, KP], BF16, name="vrows")
         nc.vector.memset(vrows[:], 0.0)
-        for v, vec_in in enumerate((b, gamma, beta)):
-            nc.scalar.dma_start(out=vrows[16 * v : 16 * v + 16, :], in_=vec_in.rearrange("k (h c) -> (k h) c", c=KP))
+        for v, vector in enumerate((b, beta, gamma)):
+            nc.scalar.dma_start(out=vrows[UNITS * v : UNITS * (v + 1), :], in_=vector.rearrange("k (h c) -> (k h) c", c=KP))
 
-        wbytes = {}
+        wrows = {}
 
-        def load_w(k, g, halves):
-            src = W_bytes[k].rearrange("(g p t) o -> g p t o", p=P, t=T)[g]
-            cols = slice(KP * halves[0], KP * (halves[-1] + 1))
-            if len(halves) == 1:
-                wb = keep.tile([P, T, KP], U8, name="wb_first%d_%d" % (g, halves[0]))
-                wbytes[2 * k + halves[0], g] = wb[:]
-            else:
-                wb = wpool.tile([P, T, DO], U8, name="wb%d" % g)
-                wbytes[2 * k, g] = wb[:]
-                wbytes[2 * k + 1, g] = wb[:, :, KP:DO]
-            nc.sync.dma_start(out=wb[:], in_=src[:, :, cols])
+        def load_w(tile, unit, g, rows, channels):
+            c0 = KP * (unit % 2)
+            src = W_bytes[unit // 2].rearrange("(g p j) o -> g p j o", p=P, j=T)[g]
+            nc.sync.dma_start(out=tile[:], in_=src[:, rows[0] : rows[-1] + 1, c0 : c0 + channels])
+            for n, j in enumerate(rows):
+                for later in range(channels // KP):
+                    wrows[unit + later, g, j] = tile[:, n, KP * later : channels]
+
+        def load_unit(unit, g, rows=range(T)):
+            load_w(keep.tile([P, len(rows), KP], U8, name="wb_unit%d_%d_%d" % (unit, g, rows[0])), unit, g, rows, KP)
+
+        def load_branch(k, passes):
+            for g in passes:
+                load_w(wpool.tile([P, T, DO], U8, name="wb%d" % g), 2 * k, g, range(T), DO)
 
         x_sb = keep.tile([P, 2, DI], BF16, name="x_sb")
         wf = keep.tile([P, UNITS, 2 * DO], U8, name="wf", align_bytes=64)
         wfs = keep.tile([P, UNITS, DO], U8, name="wfs", align_bytes=64)
         bf1_b = keep.tile([P, DO], BF16, name="bf1_b")
 
-        load_w(0, 1, (0,))
-        load_w(0, 0, (0,))
+        load_unit(0, 1, (0, 1))
+        load_unit(0, 1, (2, 3))
+        load_unit(0, 0)
         nc.sync.dma_start(out=x_sb[:], in_=x.rearrange("(r p) k -> p r k", p=P))
-        load_w(0, 1, (1,))
-        load_w(0, 0, (1,))
-        load_w(1, 0, (0, 1))
-        load_w(1, 1, (0, 1))
+        load_unit(1, 1)
+        load_unit(1, 0)
+        load_branch(1, (1, 0))
 
         ident = keep.tile([P, P], F32, name="ident")
         make_identity(nc, ident[:])
@@ -82,24 +90,22 @@ def tile_extremeoptimizationlayer_pa_w4_kernel(tc, x, W_bytes, W_scale, b, gamma
         nc.scalar.activation(eps[:], eps[:], ACT.Abs_reciprocal_sqrt, scale=EPS**-2)
         for q in range(4):
             nc.vector.memset(wfs[:, 4 * q : 4 * q + 4, :].rearrange("p u n -> p (u n)").bitcast(I32), 0)
-
         for q in range(4):
             nc.sync.dma_start(
                 out=wfs[32 * q : 32 * q + 4].bitcast(I32),
                 in_=Wf1_scales[:, 4 * q : 4 * q + 4, :].rearrange("u q n -> q u n").bitcast(I32),
             )
-        for k in range(2, 6):
-            u = slice(4 * (k - 2), 4 * (k - 2) + 4)
-            if k < 5:
-                load_w(k, 0, (0, 1))
-                load_w(k, 1, (0, 1))
-            nc.sync.dma_start(out=wf[:, u], in_=Wf1_words[u].rearrange("u p n -> p u n"))
+        for piece in range(4):
+            if 2 + piece <= W_BUFS:
+                load_branch(2 + piece, (0, 1))
+            units = slice(4 * piece, 4 * piece + 4)
+            nc.sync.dma_start(out=wf[:, units], in_=Wf1_words[units].rearrange("u p n -> p u n"))
         nc.sync.dma_start(out=bf1_b[:], in_=bf1.partition_broadcast(P))
 
         x_codes = keep.tile([P, NG, B], U32, name="x_codes", align_bytes=64)
         x_scales = keep.tile([P, NG, B], U8, name="x_scales", align_bytes=64)
         x_grouped = keep.tile([P, NG, B, T], BF16, name="x_grouped", align_bytes=64)
-        vec = keep.tile([P, 3 * UNITS, T], F32, name="vec")
+        shifts = keep.tile([P, 2, UNITS, T], F32, name="shifts")
         gain = keep.tile([P, UNITS, 2, T], F32, name="gain")
 
         def turn_x():
@@ -109,136 +115,119 @@ def tile_extremeoptimizationlayer_pa_w4_kernel(tc, x, W_bytes, W_scale, b, gamma
                 for r in range(2):
                     for u in range(2):
                         nc.tensor.transpose(xt[:, r, u, :], x_words[:, r, 256 * g + u : 256 * (g + 1) : 2], ident[:])
-                dst = x_grouped[:, g].bitcast(F32).rearrange("p (r n) u -> p r n u", r=2)
-                nc.scalar.copy(dst, xt[:].rearrange("p r u n -> p r n u"))
+                on_scalar(x_grouped[:, g].bitcast(F32).rearrange("p (r n) u -> p r n u", r=2), xt[:].rearrange("p r u n -> p r n u"))
 
         def turn_vectors():
             vt = hps.tile([P, 2, P], F32, name="h")
             for u in range(2):
                 nc.tensor.transpose(vt[:, u, :], vrows[:].bitcast(F32)[:, u::2], ident[:])
-            halves = vt[:].bitcast(BF16).rearrange("p u (r e) -> p r u e", e=2)
-            nc.scalar.copy(vec[:].rearrange("p r (u e) -> p r u e", e=2), halves[:, 0 : 3 * UNITS])
-            nc.scalar.copy(gain[:, :, 0, :].rearrange("p r (u e) -> p r u e", e=2), halves[:, UNITS : 2 * UNITS])
+            values = vt[:].bitcast(BF16).rearrange("p u (r e) -> p r u e", e=2)
+            on_scalar(shifts[:].rearrange("p v r (u e) -> p (v r) u e", e=2), values[:, 0 : 2 * UNITS])
+            on_scalar(gain[:, :, 0, :].rearrange("p r (u e) -> p r u e", e=2), values[:, 2 * UNITS : 3 * UNITS])
 
         def quant_x():
             nc.vector.quantize_mx(
                 x_codes[:].rearrange("p g n -> p (g n)").bitcast(FP8X4),
                 x_scales[:].rearrange("p g n -> p (g n)"),
-                x_grouped[:].rearrange("p g n t -> p (g n t)"),
+                x_grouped[:].rearrange("p g n j -> p (g n j)"),
             )
 
-        acc = {}
-        for m in range(2):
-            for n in range(2):
-                acc[m, n] = accps.tile([P, KP], F32, name="acc%d%d" % (m, n))
+        plane, wide, grouped, woven, codes, scales = ({} for n in range(6))
 
-        plane, whole, grouped, woven, codes, scales = ({} for n in range(6))
-        h, a, nplane, ngrp, act_codes, act_scales, pair = ({} for n in range(7))
+        def scale_row(dst, i, g, j, units):
+            row = wrows[i, g, j][:, 0 : KP * units]
+            nc.vector.tensor_scalar(dst, row.bitcast(FP8), kscale[:, g * T + j : g * T + j + 1], None, op0=ALU.mult)
 
-        def widen(i, g, units, rows=range(T)):
-            if (i, g) not in plane:
-                tile = work.tile([P, T, DO], BF16, name="plane%d" % g, align_bytes=64)
+        def widen(i, g, units):
+            tile = work.tile([P, T, DO], BF16, name="plane%d" % g, align_bytes=64)
+            for n in range(units):
+                plane[i + n, g] = tile[:, :, KP * n : KP * (n + 1)]
+            for j in range(T):
+                scale_row(tile[:, j, 0 : KP * units], i, g, j, units)
+
+        def widen_pairs(i, g, units, rows=EVEN_ROWS + ODD_ROWS):
+            if (i, g) not in wide:
+                wide[i, g] = work.tile([P, 2, DO, 2], BF16, name="plane%d" % g, align_bytes=64)
                 for n in range(units):
-                    plane[i + n, g] = tile[:, :, KP * n : KP * (n + 1)]
-                whole[i, g] = tile[:, :, 0 : KP * units]
+                    plane[i + n, g] = wide[i, g][:, :, KP * n : KP * (n + 1), :]
             for j in rows:
-                nc.vector.tensor_scalar(
-                    whole[i, g][:, j, :], wbytes[i, g][:, j, 0 : KP * units].bitcast(FP8), kscale[:, g * T + j : g * T + j + 1], None, op0=ALU.mult
-                )
-
-        def widen_pairs(i, g, units, rows=(0, 2, 1, 3)):
-            if (i, g) not in plane:
-                tile = work.tile([P, 2, DO, 2], BF16, name="plane%d" % g, align_bytes=64)
-                for n in range(units):
-                    plane[i + n, g] = tile[:, :, KP * n : KP * (n + 1), :]
-                whole[i, g] = tile[:, :, 0 : KP * units, :]
-            for j in rows:
-                nc.vector.tensor_scalar(
-                    whole[i, g][:, j // 2, :, j % 2],
-                    wbytes[i, g][:, j, 0 : KP * units].bitcast(FP8),
-                    kscale[:, g * T + j : g * T + j + 1],
-                    None,
-                    op0=ALU.mult,
-                )
+                scale_row(wide[i, g][:, j // 2, 0 : KP * units, j % 2], i, g, j, units)
 
         def group_tile(i, g):
             if i not in grouped:
                 grouped[i] = work.tile([P, NG, T, P, T], BF16, name="grouped", align_bytes=64)
             return grouped[i][:, g]
 
-        def lay_out(i, g):
-            dst = group_tile(i, g).rearrange("p t (q e) j -> p q t j e", e=2)
-            src = plane[i, g].rearrange("p j (q e t) -> p q t j e", e=2, t=T)
-            nc.scalar.copy(dst, src)
+        def lay_out(i, g, m0=0):
+            dst = group_tile(i, g)[:, :, m0:P, :].rearrange("p t (q e) j -> p q t j e", e=2)
+            on_scalar(dst, plane[i, g][:, :, T * m0 : KP].rearrange("p j (q e t) -> p q t j e", e=2, t=T))
 
-        def merge(i, g, copy=nc.scalar.copy):
+        def merge(i, g, copy=on_scalar):
             dst = group_tile(i, g).bitcast(F32).rearrange("p t m u -> p m t u")
-            src = plane[i, g].bitcast(F32).rearrange("p u (m t) z -> p m t (u z)", t=T)
-            copy(dst, src)
+            copy(dst, plane[i, g].bitcast(F32).rearrange("p u (m t) z -> p m t (u z)", t=T))
 
-        def weave(i):
+        def weave(i, quads=BANK_QUADS):
             for bank in range(2):
-                woven[i, bank] = wps.tile([P, 2, 2 * P, 2], BF16, name="woven")
+                woven[i, bank] = wps.tile([P, 2, T * quads, 2], BF16, name="woven")
             for u in range(2):
                 for bank in range(2):
-                    channels = plane[i, 1][:, 2 * u : 2 * u + 2, 2 * P * bank : 2 * P * (bank + 1)]
+                    rows = plane[i, 1][:, 2 * u : 2 * u + 2, T * quads * bank : T * quads * (bank + 1)]
                     nc.tensor.matmul(
-                        woven[i, bank][:, u].rearrange("p (q c) e -> p q e c", c=8),
+                        woven[i, bank][:, u].rearrange("p (q c) e -> p q e c", c=LINE),
                         lhsT=ident16[:],
-                        rhs=channels.rearrange("p e (q c) -> p q e c", c=8),
+                        rhs=rows.rearrange("p e (q c) -> p q e c", c=LINE),
                         start=True,
                         stop=True,
                     )
 
-        def unweave(i):
+        def unweave(i, quads=BANK_QUADS):
             for bank in range(2):
-                dst = group_tile(i, 1)[:, :, 64 * bank : 64 * bank + 64, :].bitcast(F32)
-                nc.scalar.copy(dst, woven[i, bank][:].bitcast(F32).rearrange("p u (m t) z -> p t m (u z)", t=T))
+                dst = group_tile(i, 1)[:, :, quads * bank : quads * (bank + 1), :].bitcast(F32)
+                on_scalar(dst, woven[i, bank][:].bitcast(F32).rearrange("p u (m t) z -> p t m (u z)", t=T))
 
-        def quant(i, passes=range(NG)):
-            if i not in codes:
-                codes[i] = work.tile([P, NG, KP], U32, name="codes", align_bytes=64)
-                scales[i] = work.tile([P, NG, KP], U8, name="scales", align_bytes=64)
-            g = slice(passes[0], passes[-1] + 1)
+        def quant(i):
+            codes[i] = work.tile([P, NG, KP], U32, name="codes", align_bytes=64)
+            scales[i] = work.tile([P, NG, KP], U8, name="scales", align_bytes=64)
             nc.vector.quantize_mx(
-                codes[i][:, g].rearrange("p g c -> p (g c)").bitcast(FP8X4),
-                scales[i][:, g].rearrange("p g c -> p (g c)"),
-                grouped[i][:, g].rearrange("p g t m j -> p (g t m j)"),
+                codes[i][:].rearrange("p g c -> p (g c)").bitcast(FP8X4),
+                scales[i][:].rearrange("p g c -> p (g c)"),
+                grouped[i][:].rearrange("p g t m j -> p (g t m j)"),
             )
 
-        def mm1(i):
-            for half in range(2):
-                h[i, half] = hps.tile([P, 2, B], F32, name="h")
-                for s in range(2):
-                    c = slice(P * (2 * half + s), P * (2 * half + s + 1))
-                    for g in (1, 0):
-                        nc.tensor.matmul_mx(
-                            h[i, half][:, s, :],
-                            lhsT=codes[i][:, g, c].bitcast(FP8X4),
-                            lhsT_scale=scales[i][:, g, c],
-                            rhs=x_codes[:, g, :].bitcast(FP8X4),
-                            rhs_scale=x_scales[:, g, :],
-                            start=(g == 1),
-                            stop=(g == 0),
-                        )
-
+        h, a, npairs, fused, fused_codes, fused_scales, both = ({} for n in range(7))
         sums = keep.tile([P, UNITS, T], F32, name="sums")
         squares = keep.tile([P, UNITS, T], F32, name="squares")
         rstd = keep.tile([P, UNITS, 1, T], F32, name="rstd")
         slopes = keep.tile([P, UNITS, 2, T], F32, name="slopes")
         offsets = keep.tile([P, UNITS, T], F32, name="offsets")
 
-        def relu(i, rows=range(T)):
+        def mm1(i):
+            for bank in range(2):
+                h[i, bank] = hps.tile([P, 2, B], F32, name="h")
+                for t in (2 * bank, 2 * bank + 1):
+                    cols = slice(P * t, P * (t + 1))
+                    for g in (1, 0):
+                        nc.tensor.matmul_mx(
+                            h[i, bank][:, t % 2, :],
+                            lhsT=codes[i][:, g, cols].bitcast(FP8X4),
+                            lhsT_scale=scales[i][:, g, cols],
+                            rhs=x_codes[:, g, :].bitcast(FP8X4),
+                            rhs_scale=x_scales[:, g, :],
+                            start=(g == 1),
+                            stop=(g == 0),
+                        )
+
+        def relu(i, products=range(T)):
             if i not in a:
-                a[i] = deep.tile([P, T, B], F32, name="a")
-            for t in rows:
-                nc.scalar.activation(a[i][:, t, :], h[i, t // 2][:, t % 2, :], ACT.Relu, bias=vec[:, i, t : t + 1], accum_out=sums[:, i, t : t + 1])
+                a[i] = apool.tile([P, T, B], F32, name="a")
+            for t in products:
+                nc.scalar.activation(a[i][:, t, :], h[i, t // 2][:, t % 2, :], ACT.Relu, bias=shifts[:, 0, i, t : t + 1], accum_out=sums[:, i, t : t + 1])
 
         def square(i):
-            junk = work.tile([P, T, B], BF16, name="junk")
+            terms = work.tile([P, T, B], BF16, name="terms")
             for t in range(T):
                 nc.scalar.activation(
-                    junk[:, t, :], a[i][:, t, :], ACT.Square, bias=sums[:, i, t : t + 1], scale=-float(B), accum_out=squares[:, i, t : t + 1]
+                    terms[:, t, :], a[i][:, t, :], ACT.Square, bias=sums[:, i, t : t + 1], scale=-float(B), accum_out=squares[:, i, t : t + 1]
                 )
 
         def root(i, units):
@@ -255,40 +244,54 @@ def tile_extremeoptimizationlayer_pa_w4_kernel(tc, x, W_bytes, W_scale, b, gamma
 
         def offset(i, units):
             u = slice(i, i + units)
-            nc.vector.tensor_tensor(offsets[:, u], slopes[:, u, 1, :], vec[:, 2 * UNITS + i : 2 * UNITS + i + units, :], op=ALU.add)
+            nc.vector.tensor_tensor(offsets[:, u], slopes[:, u, 1, :], shifts[:, 1, u], op=ALU.add)
 
-        def norm(i, rows=(0, 2, 1, 3)):
-            if i not in nplane:
-                nplane[i] = work.tile([P, 2, B, 2], BF16, name="nplane", align_bytes=64)
-            for t in rows:
+        def normalise(dst, i, products, rows):
+            for t in products:
                 nc.vector.tensor_scalar(
-                    nplane[i][:, t // 2, :, t % 2], a[i][:, t, :], slopes[:, i, 0, t : t + 1], offsets[:, i, t : t + 1], op0=ALU.mult, op1=ALU.add
+                    dst[:, t // 2, :, t % 2], a[i][:, t, rows], slopes[:, i, 0, t : t + 1], offsets[:, i, t : t + 1], op0=ALU.mult, op1=ALU.add
                 )
 
-        def pair_tiles(i):
+        def norm(i, products=EVEN_ROWS + ODD_ROWS):
+            if i not in npairs:
+                npairs[i] = work.tile([P, 2, B, 2], BF16, name="npairs", align_bytes=64)
+            normalise(npairs[i], i, products, slice(0, B))
+
+        def norm_both(i):
+            for products in (EVEN_ROWS, ODD_ROWS):
+                norm(i, products)
+                norm(i + 1, products)
+
+        def branch_tiles(i):
             first = i - i % 2
-            if first not in ngrp:
-                tiles = (
-                    work.tile([P, 2, B, T], BF16, name="ngrp", align_bytes=64),
-                    work.tile([P, 2, B], U32, name="act_codes", align_bytes=64),
-                    work.tile([P, 2, B], U8, name="act_scales", align_bytes=64),
+            if first not in both:
+                both[first] = (
+                    work.tile([P, 2, B, T], BF16, name="fused", align_bytes=64),
+                    work.tile([P, 2, B], U32, name="fused_codes", align_bytes=64),
+                    work.tile([P, 2, B], U8, name="fused_scales", align_bytes=64),
                 )
                 for n in range(2):
-                    ngrp[first + n], act_codes[first + n], act_scales[first + n] = (tile[:, n] for tile in tiles)
-                pair[first] = tiles
+                    fused[first + n], fused_codes[first + n], fused_scales[first + n] = (tile[:, n] for tile in both[first])
 
         def nmerge(i, copy):
-            pair_tiles(i)
-            copy(ngrp[i].bitcast(F32), nplane[i][:].bitcast(F32).rearrange("p u n z -> p n (u z)"))
+            branch_tiles(i)
+            copy(fused[i].bitcast(F32), npairs[i][:].bitcast(F32).rearrange("p u n z -> p n (u z)"))
 
-        def nquant(i):
-            nc.vector.quantize_mx(act_codes[i].bitcast(FP8X4), act_scales[i], ngrp[i].rearrange("p n t -> p (n t)"))
+        def nquant(i, rows=slice(0, B)):
+            nc.vector.quantize_mx(fused_codes[i][:, rows].bitcast(FP8X4), fused_scales[i][:, rows], fused[i][:, rows].rearrange("p n t -> p (n t)"))
 
-        def nquant_pair(i):
-            values, words, bytes_ = pair[i]
+        def nquant_both(i):
+            values, words, exponents = both[i]
             nc.vector.quantize_mx(
-                words[:].rearrange("p u n -> p (u n)").bitcast(FP8X4), bytes_[:].rearrange("p u n -> p (u n)"), values[:].rearrange("p u n t -> p (u n t)")
+                words[:].rearrange("p u n -> p (u n)").bitcast(FP8X4),
+                exponents[:].rearrange("p u n -> p (u n)"),
+                values[:].rearrange("p u n t -> p (u n t)"),
             )
+
+        acc = {}
+        for m in range(2):
+            for n in range(2):
+                acc[m, n] = accps.tile([P, KP], F32, name="acc%d%d" % (m, n))
 
         def mm2(i, halves=(0, 1)):
             for m in halves:
@@ -296,171 +299,157 @@ def tile_extremeoptimizationlayer_pa_w4_kernel(tc, x, W_bytes, W_scale, b, gamma
                 for n in range(2):
                     nc.tensor.matmul_mx(
                         acc[m, n][:],
-                        lhsT=act_codes[i][:, rows].bitcast(FP8X4),
-                        lhsT_scale=act_scales[i][:, rows],
+                        lhsT=fused_codes[i][:, rows].bitcast(FP8X4),
+                        lhsT_scale=fused_scales[i][:, rows],
                         rhs=wf[:, i, DO * n : DO * (n + 1)].bitcast(FP4X4),
                         rhs_scale=wfs[:, i, KP * n : KP * (n + 1)],
                         start=(i == 0),
-                        stop=(i == UNITS - 1),
+                        stop=(i == LAST),
                     )
-
-        def when(f, i, *args):
-            if i >= 0:
-                f(i, *args)
-
-        def lay_out_pass1(s):
-            if s < PAIRED:
-                merge(s, 1)
-            else:
-                unweave(s)
 
         widen(0, 1, 1)
         lay_out(0, 1)
+        turn_vectors()
         widen_pairs(0, 0, 1)
         merge(0, 0)
         widen(1, 1, 1)
         turn_x()
+        weave(1, SPARE_QUADS)
         widen_pairs(1, 0, 1)
-        lay_out(1, 1)
-        turn_vectors()
+        lay_out(1, 1, 2 * SPARE_QUADS)
+        unweave(1, SPARE_QUADS)
         quant_x()
         quant(0)
         mm1(0)
         merge(1, 0)
-        widen_pairs(2, 0, 2)
+        widen(2, 1, 2)
+        weave(2)
 
         for s in range(2, UNITS - 2, 2):
-            if s < PAIRED:
-                widen_pairs(s, 1, 1)
+            first = s == 2
+            relu(s - 2)
+            if first:
+                widen_pairs(s, 0, 1)
             else:
                 widen(s, 1, 2)
-            relu(s - 2)
-            if s >= PAIRED:
                 weave(s)
-            when(norm, s - 4)
             square(s - 2)
             quant(s - 1)
             mm1(s - 1)
-            when(mm2, s - 6)
-            merge(s, 0)
-            if s >= 4:
-                norm(s - 3)
-            when(nmerge, s - 4, nc.scalar.copy)
-            lay_out_pass1(s)
-            if 5 <= s // 2 + 3 < NB:
-                load_w(s // 2 + 3, 0, (0, 1))
-                load_w(s // 2 + 3, 1, (0, 1))
-            o = s + 1
-            relu(o - 2)
-            if o >= PAIRED:
-                weave(o)
+            if s >= 6:
+                mm2(s - 6)
+            if first:
+                unweave(s)
+                merge(s, 0)
+                widen_pairs(s + 1, 0, 1)
             else:
-                widen_pairs(o, 1, 1)
-            widen_pairs(o + 1, 0, 2, (0, 2))
-            square(o - 2)
-            if s >= 4:
-                nmerge(s - 3, nc.vector.tensor_copy)
-            quant(o - 1)
-            mm1(o - 1)
+                merge(s, 0)
+                norm_both(s - 4)
+                unweave(s)
+            ahead = s // 2 + W_BUFS - 1
+            if W_BUFS < ahead < NB:
+                load_branch(ahead, (0, 1))
+
+            relu(s - 1)
+            if not first:
+                nmerge(s - 4, on_scalar)
+            weave(s + 1)
+            widen_pairs(s + 2, 0, 2, EVEN_ROWS)
+            square(s - 1)
+            if not first:
+                nmerge(s - 3, on_vector)
+            quant(s)
+            mm1(s)
             if s >= 6:
                 mm2(s - 5)
             centre(s - 2, 2)
-            widen_pairs(o + 1, 0, 2, (1,))
-            merge(o, 0)
+            widen_pairs(s + 2, 0, 2, ODD_ROWS[:1])
+            merge(s + 1, 0)
             root(s - 2, 2)
-            widen_pairs(o + 1, 0, 2, (3,))
+            widen_pairs(s + 2, 0, 2, ODD_ROWS[1:])
             slope(s - 2, 2)
-            when(nquant_pair, s - 4)
+            if not first:
+                nquant_both(s - 4)
             offset(s - 2, 2)
-            lay_out_pass1(o)
+            unweave(s + 1)
 
-        def norm_half(i, m):
-            pair_tiles(i)
-            nplane[i, m] = keep.tile([P, 2, P, 2], BF16, name="nplane_half%d" % m, align_bytes=64)
-            rows = slice(P * m, P * (m + 1))
-            for t in (0, 2, 1, 3):
-                nc.vector.tensor_scalar(
-                    nplane[i, m][:, t // 2, :, t % 2], a[i][:, t, rows], slopes[:, i, 0, t : t + 1], offsets[:, i, t : t + 1], op0=ALU.mult, op1=ALU.add
-                )
+        s = UNITS - 2
+        widen_pairs(s, 1, 2, EVEN_ROWS)
+        relu(s - 2)
+        quant(s - 1)
+        mm1(s - 1)
+        mm2(s - 6)
+        mm2(s - 5)
+        widen_pairs(s, 1, 2, ODD_ROWS)
+        square(s - 2)
+        merge(s, 0)
+        norm(s - 4, EVEN_ROWS)
+        norm(s - 3, EVEN_ROWS)
+        merge(s, 1, on_vector)
+        norm(s - 4, ODD_ROWS)
+        relu(s - 1)
+        quant(s)
+        mm1(s)
+        merge(s + 1, 0)
+        merge(s + 1, 1)
+        norm(s - 3, ODD_ROWS)
+        nmerge(s - 4, on_vector)
+        square(s - 1)
+        nmerge(s - 3, on_vector)
+        nquant(s - 4)
+        mm2(s - 4)
+        quant(s + 1)
+        centre(s - 2, 2)
+        relu(s, (0,))
+        root(s - 2, 2)
+        relu(s, (1, 2, 3))
+        nquant(s - 3)
+        mm1(s + 1)
+        mm2(s - 3)
+        slope(s - 2, 2)
+        square(s)
+        offset(s - 2, 2)
+        centre(s, 1)
+        norm(s - 2, EVEN_ROWS)
+        norm(s - 1, EVEN_ROWS)
+        relu(s + 1, (0,))
+        root(s, 1)
+        relu(s + 1, (1, 2, 3))
+        norm(s - 2, ODD_ROWS)
+        norm(s - 1, ODD_ROWS)
+        square(s + 1)
+        nmerge(s - 2, on_vector)
+        slope(s, 1)
+        nmerge(s - 1, on_vector)
+        offset(s, 1)
+        nquant(s - 2)
+        mm2(s - 2)
+        centre(s + 1, 1)
+        nquant(s - 1)
+        mm2(s - 1)
+        norm(s)
+        root(s + 1, 1)
+        nmerge(s, on_scalar)
+        slope(s + 1, 1)
+        offset(s + 1, 1)
 
-        def nmerge_half(i, m, copy):
-            rows = slice(P * m, P * (m + 1))
-            copy(ngrp[i][:, rows].bitcast(F32), nplane[i, m][:].bitcast(F32).rearrange("p u n z -> p n (u z)"))
-
-        def nquant_half(i, m):
-            rows = slice(P * m, P * (m + 1))
-            nc.vector.quantize_mx(act_codes[i][:, rows].bitcast(FP8X4), act_scales[i][:, rows], ngrp[i][:, rows].rearrange("p n t -> p (n t)"))
-
-        widen_pairs(14, 1, 2, (0, 2))
-        relu(12)
-        quant(13)
-        mm1(13)
-        mm2(8)
-        mm2(9)
-        widen_pairs(14, 1, 2, (1, 3))
-        square(12)
-        merge(14, 0)
-        norm(10)
-        merge(14, 1, nc.vector.tensor_copy)
-        relu(13)
-        quant(14)
-        mm1(14)
-        merge(15, 0)
-        merge(15, 1)
-        norm(11)
-        nmerge(10, nc.vector.tensor_copy)
-        square(13)
-        quant(15)
-        nmerge(11, nc.vector.tensor_copy)
-        centre(12, 2)
-        relu(14, (0,))
-        root(12, 2)
-        relu(14, (1, 2, 3))
-        mm1(15)
-        nquant_pair(10)
-        mm2(10)
-        mm2(11)
-        slope(12, 2)
-        square(14)
-        offset(12, 2)
-        centre(14, 1)
-        norm(12)
-        relu(15, (0,))
-        root(14, 1)
-        relu(15, (1, 2, 3))
-        norm(13)
-        nmerge(12, nc.vector.tensor_copy)
-        square(15)
-        slope(14, 1)
-        nmerge(13, nc.vector.tensor_copy)
-        offset(14, 1)
-        nquant(12)
-        mm2(12)
-        centre(LAST, 1)
-        nquant(13)
-        mm2(13)
-        norm(14)
-        root(LAST, 1)
-        nmerge(14, nc.scalar.copy)
-        slope(LAST, 1)
-        offset(LAST, 1)
-        norm_half(LAST, 0)
-        nquant(14)
-        nmerge_half(LAST, 0, nc.scalar.copy)
-        norm_half(LAST, 1)
-        nmerge_half(LAST, 1, nc.scalar.copy)
-        mm2(14, (0,))
-        nquant_half(LAST, 0)
-        mm2(LAST, (0,))
-        mm2(14, (1,))
-        nquant_half(LAST, 1)
-        mm2(LAST, (1,))
+        halves = [slice(P * m, P * (m + 1)) for m in range(2)]
+        for m in range(2):
+            last_pairs = keep.tile([P, 2, P, 2], BF16, name="last_pairs%d" % m, align_bytes=64)
+            normalise(last_pairs, LAST, EVEN_ROWS + ODD_ROWS, halves[m])
+            if m == 0:
+                nquant(s)
+            on_scalar(fused[LAST][:, halves[m]].bitcast(F32), last_pairs[:].bitcast(F32).rearrange("p u n z -> p n (u z)"))
+        for m in range(2):
+            mm2(s, (m,))
+            nquant(LAST, halves[m])
+            mm2(LAST, (m,))
 
         pieces = [(0, 0, KP), (0, KP, KP), (1, 0, KP), (1, KP, KP // 2), (1, KP + KP // 2, KP // 2)]
         for m, c0, width in pieces:
             cols = slice(c0, c0 + width)
-            z = keep.tile([P, width], F32, name="z%d_%d" % (m, c0))
-            nc.vector.tensor_tensor(z[:], acc[m, c0 // KP][:, c0 % KP : c0 % KP + width], bf1_b[:, cols], op=ALU.add)
-            o = keep.tile([P, width], F32, name="o%d_%d" % (m, c0))
-            nc.scalar.activation(o[:], z[:], ACT.Relu)
-            nc.sync.dma_start(out=out[P * m : P * (m + 1), cols], in_=o[:])
+            biased = keep.tile([P, width], F32, name="biased%d_%d" % (m, c0))
+            nc.vector.tensor_tensor(biased[:], acc[m, c0 // KP][:, c0 % KP : c0 % KP + width], bf1_b[:, cols], op=ALU.add)
+            result = keep.tile([P, width], F32, name="result%d_%d" % (m, c0))
+            nc.scalar.activation(result[:], biased[:], ACT.Relu)
+            nc.sync.dma_start(out=out[halves[m], cols], in_=result[:])

@@ -90,16 +90,18 @@ def tile_extremeoptimizationlayer_pa_w4_kernel(tc, x, W_bytes, W_scale, b, gamma
         nc.scalar.activation(eps[:], eps[:], ACT.Abs_reciprocal_sqrt, scale=EPS**-2)
         for q in range(4):
             nc.vector.memset(wfs[:, 4 * q : 4 * q + 4, :].rearrange("p u n -> p (u n)").bitcast(I32), 0)
+        for k in range(2, W_BUFS):
+            load_branch(k, (0, 1))
         for q in range(4):
             nc.sync.dma_start(
                 out=wfs[32 * q : 32 * q + 4].bitcast(I32),
                 in_=Wf1_scales[:, 4 * q : 4 * q + 4, :].rearrange("u q n -> q u n").bitcast(I32),
             )
         for piece in range(4):
-            if 2 + piece <= W_BUFS:
-                load_branch(2 + piece, (0, 1))
             units = slice(4 * piece, 4 * piece + 4)
             nc.sync.dma_start(out=wf[:, units], in_=Wf1_words[units].rearrange("u p n -> p u n"))
+            if piece == 0:
+                load_branch(W_BUFS, (0, 1))
         nc.sync.dma_start(out=bf1_b[:], in_=bf1.partition_broadcast(P))
 
         x_codes = keep.tile([P, NG, B], U32, name="x_codes", align_bytes=64)
@@ -334,6 +336,8 @@ def tile_extremeoptimizationlayer_pa_w4_kernel(tc, x, W_bytes, W_scale, b, gamma
                 widen(s, 1, 2)
                 weave(s)
             square(s - 2)
+            if not first:
+                offset(s - 4, 2)
             quant(s - 1)
             mm1(s - 1)
             if s >= 6:
@@ -351,31 +355,33 @@ def tile_extremeoptimizationlayer_pa_w4_kernel(tc, x, W_bytes, W_scale, b, gamma
                 load_branch(ahead, (0, 1))
 
             relu(s - 1)
-            if not first:
-                nmerge(s - 4, on_scalar)
             weave(s + 1)
             widen_pairs(s + 2, 0, 2, EVEN_ROWS)
             square(s - 1)
             if not first:
-                nmerge(s - 3, on_vector)
+                nmerge(s - 4, on_scalar)
+                nmerge(s - 3, on_scalar)
             quant(s)
             mm1(s)
             if s >= 6:
                 mm2(s - 5)
             centre(s - 2, 2)
             widen_pairs(s + 2, 0, 2, ODD_ROWS[:1])
-            merge(s + 1, 0)
+            if first:
+                merge(s + 1, 0)
             root(s - 2, 2)
+            if not first:
+                merge(s + 1, 0)
             widen_pairs(s + 2, 0, 2, ODD_ROWS[1:])
-            slope(s - 2, 2)
             if not first:
                 nquant_both(s - 4)
-            offset(s - 2, 2)
+            slope(s - 2, 2)
             unweave(s + 1)
 
         s = UNITS - 2
         widen_pairs(s, 1, 2, EVEN_ROWS)
         relu(s - 2)
+        offset(s - 4, 2)
         quant(s - 1)
         mm1(s - 1)
         mm2(s - 6)

@@ -25,6 +25,7 @@ EPS = 1e-5
 BANK_QUADS = 64
 SPARE_QUADS = 48
 LINE = 8
+SCALE_SLOTS = 8
 W_BUFS = 4
 EVEN_ROWS, ODD_ROWS = (0, 2), (1, 3)
 
@@ -70,14 +71,14 @@ def tile_extremeoptimizationlayer_pa_w4_kernel(tc, x, W_bytes, W_scale, b, gamma
 
         x_sb = keep.tile([P, 2, DI], BF16, name="x_sb")
         wf = keep.tile([P, UNITS, 2 * DO], U8, name="wf", align_bytes=64)
-        wfs = keep.tile([P, UNITS, DO], U8, name="wfs", align_bytes=64)
+        wfs = keep.tile([P, SCALE_SLOTS, DO], U8, name="wfs", align_bytes=64)
         bf1_b = keep.tile([P, DO], BF16, name="bf1_b")
 
         load_unit(0, 1, (0, 1))
         load_unit(0, 1, (2, 3))
         load_unit(0, 0)
-        nc.sync.dma_start(out=x_sb[:], in_=x.rearrange("(r p) k -> p r k", p=P))
         load_unit(1, 1)
+        nc.sync.dma_start(out=x_sb[:], in_=x.rearrange("(r p) k -> p r k", p=P))
         load_unit(1, 0)
         load_branch(1, (1, 0))
 
@@ -88,15 +89,20 @@ def tile_extremeoptimizationlayer_pa_w4_kernel(tc, x, W_bytes, W_scale, b, gamma
         eps = keep.tile([P, 1], F32, name="eps")
         nc.vector.memset(eps[:], 1.0)
         nc.scalar.activation(eps[:], eps[:], ACT.Abs_reciprocal_sqrt, scale=EPS**-2)
-        for q in range(4):
-            nc.vector.memset(wfs[:, 4 * q : 4 * q + 4, :].rearrange("p u n -> p (u n)").bitcast(I32), 0)
+        for slot in range(0, SCALE_SLOTS, 4):
+            nc.vector.memset(wfs[:, slot : slot + 4, :].rearrange("p u n -> p (u n)").bitcast(I32), 0)
+
+        def load_scales(unit, units):
+            slot = unit % SCALE_SLOTS
+            for q in range(4):
+                nc.sync.dma_start(
+                    out=wfs[32 * q : 32 * q + 4, slot : slot + units].bitcast(I32),
+                    in_=Wf1_scales[unit : unit + units, 4 * q : 4 * q + 4, :].rearrange("u q n -> q u n").bitcast(I32),
+                )
+
         for k in range(2, W_BUFS):
             load_branch(k, (0, 1))
-        for q in range(4):
-            nc.sync.dma_start(
-                out=wfs[32 * q : 32 * q + 4].bitcast(I32),
-                in_=Wf1_scales[:, 4 * q : 4 * q + 4, :].rearrange("u q n -> q u n").bitcast(I32),
-            )
+        load_scales(0, SCALE_SLOTS)
         for piece in range(4):
             units = slice(4 * piece, 4 * piece + 4)
             nc.sync.dma_start(out=wf[:, units], in_=Wf1_words[units].rearrange("u p n -> p u n"))
@@ -304,7 +310,7 @@ def tile_extremeoptimizationlayer_pa_w4_kernel(tc, x, W_bytes, W_scale, b, gamma
                         lhsT=fused_codes[i][:, rows].bitcast(FP8X4),
                         lhsT_scale=fused_scales[i][:, rows],
                         rhs=wf[:, i, DO * n : DO * (n + 1)].bitcast(FP4X4),
-                        rhs_scale=wfs[:, i, KP * n : KP * (n + 1)],
+                        rhs_scale=wfs[:, i % SCALE_SLOTS, KP * n : KP * (n + 1)],
                         start=(i == 0),
                         stop=(i == LAST),
                     )
@@ -365,6 +371,8 @@ def tile_extremeoptimizationlayer_pa_w4_kernel(tc, x, W_bytes, W_scale, b, gamma
             mm1(s)
             if s >= 6:
                 mm2(s - 5)
+            if s >= 8 and s % 4 == 0:
+                load_scales(s, 4)
             centre(s - 2, 2)
             widen_pairs(s + 2, 0, 2, ODD_ROWS[:1])
             if first:
@@ -458,4 +466,5 @@ def tile_extremeoptimizationlayer_pa_w4_kernel(tc, x, W_bytes, W_scale, b, gamma
             nc.vector.tensor_tensor(biased[:], acc[m, c0 // KP][:, c0 % KP : c0 % KP + width], bf1_b[:, cols], op=ALU.add)
             result = keep.tile([P, width], F32, name="result%d_%d" % (m, c0))
             nc.scalar.activation(result[:], biased[:], ACT.Relu)
-            nc.sync.dma_start(out=out[halves[m], cols], in_=result[:])
+            queue = nc.scalar if c0 + width == DO and m == 1 else nc.sync
+            queue.dma_start(out=out[halves[m], cols], in_=result[:])

@@ -146,12 +146,16 @@ def tile_extremeoptimizationlayer_pa_w4_kernel(tc, x, W_bytes, W_scale, b, gamma
             row = wrows[i, g, j][:, 0 : KP * units]
             nc.vector.tensor_scalar(dst, row.bitcast(FP8), kscale[:, g * T + j : g * T + j + 1], None, op0=ALU.mult)
 
-        def widen(i, g, units):
+        def widen(i, g, units, scalar_rows=()):
             tile = work.tile([P, T, DO], BF16, name="plane%d" % g, align_bytes=64)
             for n in range(units):
                 plane[i + n, g] = tile[:, :, KP * n : KP * (n + 1)]
             for j in range(T):
-                scale_row(tile[:, j, 0 : KP * units], i, g, j, units)
+                if j in scalar_rows:
+                    row = wrows[i, g, j][:, 0 : KP * units]
+                    nc.scalar.activation(tile[:, j, 0 : KP * units], row.bitcast(FP8), ACT.Copy, scale=kscale[:, g * T + j : g * T + j + 1])
+                else:
+                    scale_row(tile[:, j, 0 : KP * units], i, g, j, units)
 
         def widen_pairs(i, g, units, rows=EVEN_ROWS + ODD_ROWS):
             if (i, g) not in wide:
@@ -315,7 +319,7 @@ def tile_extremeoptimizationlayer_pa_w4_kernel(tc, x, W_bytes, W_scale, b, gamma
                         stop=(i == LAST),
                     )
 
-        widen(0, 1, 1)
+        widen(0, 1, 1, scalar_rows=(1,))
         lay_out(0, 1)
         turn_vectors()
         widen_pairs(0, 0, 1)
@@ -459,8 +463,8 @@ def tile_extremeoptimizationlayer_pa_w4_kernel(tc, x, W_bytes, W_scale, b, gamma
             nquant(LAST, halves[m])
             mm2(LAST, (m,))
 
-        pieces = [(0, 0, KP), (0, KP, KP), (1, 0, KP), (1, KP, KP // 2), (1, KP + KP // 2, KP // 2)]
-        for m, c0, width in pieces:
+        width = KP // 2
+        for m, c0 in [(m, c0) for m in range(2) for c0 in range(0, DO, width)]:
             cols = slice(c0, c0 + width)
             biased = keep.tile([P, width], F32, name="biased%d_%d" % (m, c0))
             nc.vector.tensor_tensor(biased[:], acc[m, c0 // KP][:, c0 % KP : c0 % KP + width], bf1_b[:, cols], op=ALU.add)

@@ -351,7 +351,7 @@ def tile_extremeoptimizationlayer_pa_w4_kernel(tc, x, W_bytes, W_scale, b, gamma
             quant(s - 1)
             mm1(s - 1)
             if s >= 6:
-                mm2(s - 6)
+                mm2(s - 5)
             if first:
                 unweave(s)
                 merge(s, 0)
@@ -363,6 +363,8 @@ def tile_extremeoptimizationlayer_pa_w4_kernel(tc, x, W_bytes, W_scale, b, gamma
             ahead = s // 2 + W_BUFS - 1
             if W_BUFS < ahead < NB:
                 load_branch(ahead, (0, 1))
+            if s >= 8 and s % 4 == 0:
+                load_scales(s, 4)
 
             relu(s - 1)
             weave(s + 1)
@@ -373,10 +375,6 @@ def tile_extremeoptimizationlayer_pa_w4_kernel(tc, x, W_bytes, W_scale, b, gamma
                 nmerge(s - 3, on_scalar)
             quant(s)
             mm1(s)
-            if s >= 6:
-                mm2(s - 5)
-            if s >= 8 and s % 4 == 0:
-                load_scales(s, 4)
             centre(s - 2, 2)
             widen_pairs(s + 2, 0, 2, ODD_ROWS[:1])
             if first:
@@ -387,17 +385,18 @@ def tile_extremeoptimizationlayer_pa_w4_kernel(tc, x, W_bytes, W_scale, b, gamma
             widen_pairs(s + 2, 0, 2, ODD_ROWS[1:])
             if not first:
                 nquant_both(s - 4)
+                mm2(s - 4)
             slope(s - 2, 2)
             unweave(s + 1)
 
         s = UNITS - 2
         widen_pairs(s, 1, 2, EVEN_ROWS)
+        mm2(s - 5, (0,))
         relu(s - 2)
         offset(s - 4, 2)
         quant(s - 1)
         mm1(s - 1)
-        mm2(s - 6)
-        mm2(s - 5)
+        mm2(s - 5, (1,))
         widen_pairs(s, 1, 2, ODD_ROWS)
         square(s - 2)
         merge(s, 0)
@@ -414,18 +413,18 @@ def tile_extremeoptimizationlayer_pa_w4_kernel(tc, x, W_bytes, W_scale, b, gamma
         nmerge(s - 4, on_vector)
         square(s - 1)
         nmerge(s - 3, on_vector)
+        centre(s - 2, 2)
         nquant(s - 4)
         mm2(s - 4)
         quant(s + 1)
-        centre(s - 2, 2)
         relu(s, (0,))
         root(s - 2, 2)
         relu(s, (1, 2, 3))
-        nquant(s - 3)
         mm1(s + 1)
-        mm2(s - 3)
         slope(s - 2, 2)
         square(s)
+        nquant(s - 3)
+        mm2(s - 3)
         offset(s - 2, 2)
         centre(s, 1)
         norm(s - 2, EVEN_ROWS)
@@ -443,12 +442,12 @@ def tile_extremeoptimizationlayer_pa_w4_kernel(tc, x, W_bytes, W_scale, b, gamma
         nquant(s - 2)
         mm2(s - 2)
         centre(s + 1, 1)
-        nquant(s - 1)
-        mm2(s - 1)
         norm(s)
         root(s + 1, 1)
         nmerge(s, on_scalar)
         slope(s + 1, 1)
+        nquant(s - 1)
+        mm2(s - 1)
         offset(s + 1, 1)
 
         halves = [slice(P * m, P * (m + 1)) for m in range(2)]

@@ -77,8 +77,8 @@ def tile_extremeoptimizationlayer_pa_w4_kernel(tc, x, W_bytes, W_scale, b, gamma
         load_unit(0, 1, (0, 1))
         load_unit(0, 1, (2, 3))
         load_unit(0, 0)
-        load_unit(1, 1)
         nc.sync.dma_start(out=x_sb[:], in_=x.rearrange("(r p) k -> p r k", p=P))
+        load_unit(1, 1)
         load_unit(1, 0)
         load_branch(1, (1, 0))
 
@@ -174,9 +174,13 @@ def tile_extremeoptimizationlayer_pa_w4_kernel(tc, x, W_bytes, W_scale, b, gamma
             dst = group_tile(i, g)[:, :, m0:P, :].rearrange("p t (q e) j -> p q t j e", e=2)
             on_scalar(dst, plane[i, g][:, :, T * m0 : KP].rearrange("p j (q e t) -> p q t j e", e=2, t=T))
 
-        def merge(i, g, copy=on_scalar):
+        def merge(i, g):
             dst = group_tile(i, g).bitcast(F32).rearrange("p t m u -> p m t u")
-            copy(dst, plane[i, g].bitcast(F32).rearrange("p u (m t) z -> p m t (u z)", t=T))
+            on_scalar(dst, plane[i, g].bitcast(F32).rearrange("p u (m t) z -> p m t (u z)", t=T))
+
+        def merge_on_vector(i, g):
+            dst = group_tile(i, g).bitcast(F32).rearrange("p (s t) m u -> p m s u t", s=2)
+            on_vector(dst, plane[i, g].bitcast(F32).rearrange("p u (m s t) z -> p m s u (t z)", s=2, t=2))
 
         def weave(i, quads=BANK_QUADS):
             for bank in range(2):
@@ -287,7 +291,9 @@ def tile_extremeoptimizationlayer_pa_w4_kernel(tc, x, W_bytes, W_scale, b, gamma
 
         def nmerge(i, copy):
             branch_tiles(i)
-            copy(fused[i].bitcast(F32), npairs[i][:].bitcast(F32).rearrange("p u n z -> p n (u z)"))
+            run = 2 if copy is on_vector else 1
+            dst = fused[i].bitcast(F32).rearrange("p (q e) u -> p q u e", e=run)
+            copy(dst, npairs[i][:].bitcast(F32).rearrange("p u (q e) z -> p q u (e z)", e=run))
 
         def nquant(i, rows=slice(0, B)):
             nc.vector.quantize_mx(fused_codes[i][:, rows].bitcast(FP8X4), fused_scales[i][:, rows], fused[i][:, rows].rearrange("p n t -> p (n t)"))
@@ -329,11 +335,11 @@ def tile_extremeoptimizationlayer_pa_w4_kernel(tc, x, W_bytes, W_scale, b, gamma
         weave(1, SPARE_QUADS)
         widen_pairs(1, 0, 1)
         lay_out(1, 1, 2 * SPARE_QUADS)
+        merge(1, 0)
         unweave(1, SPARE_QUADS)
         quant_x()
         quant(0)
         mm1(0)
-        merge(1, 0)
         widen(2, 1, 2)
         weave(2)
 
@@ -402,7 +408,7 @@ def tile_extremeoptimizationlayer_pa_w4_kernel(tc, x, W_bytes, W_scale, b, gamma
         merge(s, 0)
         norm(s - 4, EVEN_ROWS)
         norm(s - 3, EVEN_ROWS)
-        merge(s, 1, on_vector)
+        merge_on_vector(s, 1)
         norm(s - 4, ODD_ROWS)
         relu(s - 1)
         quant(s)

@@ -337,8 +337,8 @@ def tile_extremeoptimizationlayer_pa_w4_kernel(tc, x, W_bytes, W_scale, b, gamma
         lay_out(1, 1, 2 * SPARE_QUADS)
         merge(1, 0)
         unweave(1, SPARE_QUADS)
-        quant_x()
         quant(0)
+        quant_x()
         mm1(0)
         widen(2, 1, 2)
         weave(2)

@@ -421,12 +421,12 @@ def tile_extremeoptimizationlayer_pa_w4_kernel(tc, x, W_bytes, W_scale, b, gamma
         nmerge(s - 3, on_vector)
         centre(s - 2, 2)
         nquant(s - 4)
-        mm2(s - 4)
         quant(s + 1)
         relu(s, (0,))
         root(s - 2, 2)
         relu(s, (1, 2, 3))
         mm1(s + 1)
+        mm2(s - 4)
         slope(s - 2, 2)
         square(s)
         nquant(s - 3)

@@ -75,10 +75,11 @@ def tile_extremeoptimizationlayer_pa_w4_kernel(tc, x, W_bytes, W_scale, b, gamma
         bf1_b = keep.tile([P, DO], BF16, name="bf1_b")
 
         load_unit(0, 1, (0, 1))
+        load_unit(1, 1, (0, 1))
         load_unit(0, 1, (2, 3))
         load_unit(0, 0)
+        load_unit(1, 1, (2, 3))
         nc.sync.dma_start(out=x_sb[:], in_=x.rearrange("(r p) k -> p r k", p=P))
-        load_unit(1, 1)
         load_unit(1, 0)
         load_branch(1, (1, 0))
 
@@ -146,11 +147,13 @@ def tile_extremeoptimizationlayer_pa_w4_kernel(tc, x, W_bytes, W_scale, b, gamma
             row = wrows[i, g, j][:, 0 : KP * units]
             nc.vector.tensor_scalar(dst, row.bitcast(FP8), kscale[:, g * T + j : g * T + j + 1], None, op0=ALU.mult)
 
-        def widen(i, g, units, scalar_rows=()):
-            tile = work.tile([P, T, DO], BF16, name="plane%d" % g, align_bytes=64)
-            for n in range(units):
-                plane[i + n, g] = tile[:, :, KP * n : KP * (n + 1)]
-            for j in range(T):
+        def widen(i, g, units, rows=range(T), scalar_rows=()):
+            if (i, g) not in wide:
+                wide[i, g] = work.tile([P, T, DO], BF16, name="plane%d" % g, align_bytes=64)
+                for n in range(units):
+                    plane[i + n, g] = wide[i, g][:, :, KP * n : KP * (n + 1)]
+            tile = wide[i, g]
+            for j in rows:
                 if j in scalar_rows:
                     row = wrows[i, g, j][:, 0 : KP * units]
                     nc.scalar.activation(tile[:, j, 0 : KP * units], row.bitcast(FP8), ACT.Copy, scale=kscale[:, g * T + j : g * T + j + 1])
@@ -325,12 +328,13 @@ def tile_extremeoptimizationlayer_pa_w4_kernel(tc, x, W_bytes, W_scale, b, gamma
                         stop=(i == LAST),
                     )
 
-        widen(0, 1, 1, scalar_rows=(1,))
-        lay_out(0, 1)
+        widen_pairs(0, 1, 1)
+        widen(1, 1, 1, (0, 1, 2), scalar_rows=(0, 1, 2))
+        merge(0, 1)
         turn_vectors()
         widen_pairs(0, 0, 1)
         merge(0, 0)
-        widen(1, 1, 1)
+        widen(1, 1, 1, (3,))
         turn_x()
         weave(1, SPARE_QUADS)
         widen_pairs(1, 0, 1)

from contextlib import ExitStack

import concourse.mybir as mybir
from concourse.masks import make_identity

F32 = mybir.dt.float32
BF16 = mybir.dt.bfloat16
I32 = mybir.dt.int32
U32 = mybir.dt.uint32
U8 = mybir.dt.uint8
FP8 = mybir.dt.float8_e4m3fn
FP8X4 = mybir.dt.float8_e4m3fn_x4
FP4X4 = mybir.dt.float4_e2m1fn_x4
ACT = mybir.ActivationFunctionType
ALU = mybir.AluOpType

NB, DI, DO, B = 8, 1024, 1024, 256
P = 128
T = 4
KP = P * T
NG = DI // KP
UNITS = NB * DO // KP
LAST = UNITS - 1
EPS = 1e-5
BANK_QUADS = 64
SPARE_QUADS = 48
LINE = 8
SCALE_SLOTS = 8
W_BUFS = 4
EVEN_ROWS, ODD_ROWS = (0, 2), (1, 3)

FLOPS = 2 * B * DI * NB * DO + 2 * B * NB * DO * DO


def tile_extremeoptimizationlayer_pa_w4_kernel(tc, x, W_bytes, W_scale, b, gamma, beta, Wf1_words, Wf1_scales, bf1, out):
    nc = tc.nc
    on_scalar, on_vector = nc.scalar.copy, nc.vector.tensor_copy
    with ExitStack() as ctx:
        keep = ctx.enter_context(tc.tile_pool(name="keep", bufs=1))
        work = ctx.enter_context(tc.tile_pool(name="work", bufs=2))
        apool = ctx.enter_context(tc.tile_pool(name="apool", bufs=4))
        wpool = ctx.enter_context(tc.tile_pool(name="wpool", bufs=W_BUFS))
        hps = ctx.enter_context(tc.psum_pool(name="hps", bufs=2))
        wps = ctx.enter_context(tc.psum_pool(name="wps", bufs=2))
        accps = ctx.enter_context(tc.psum_pool(name="accps", bufs=1))
        ctx.enter_context(tc.manual_schedule())

        kscale = keep.tile([P, NG * T], F32, name="kscale")
        nc.scalar.dma_start(out=kscale[:].rearrange("p (g j) -> p g j", g=NG), in_=W_scale.rearrange("o (g p j) z -> p (o g) (j z)", p=P, j=T))
        vrows = keep.tile([P, KP], BF16, name="vrows")
        nc.vector.memset(vrows[:], 0.0)
        for v, vector in enumerate((b, beta, gamma)):
            nc.scalar.dma_start(out=vrows[UNITS * v : UNITS * (v + 1), :], in_=vector.rearrange("k (h c) -> (k h) c", c=KP))

        wrows = {}

        def load_w(tile, unit, g, rows, channels):
            c0 = KP * (unit % 2)
            src = W_bytes[unit // 2].rearrange("(g p j) o -> g p j o", p=P, j=T)[g]
            nc.sync.dma_start(out=tile[:], in_=src[:, rows[0] : rows[-1] + 1, c0 : c0 + channels])
            for n, j in enumerate(rows):
                for later in range(channels // KP):
                    wrows[unit + later, g, j] = tile[:, n, KP * later : channels]

        def load_unit(unit, g, rows=range(T)):
            load_w(keep.tile([P, len(rows), KP], U8, name="wb_unit%d_%d_%d" % (unit, g, rows[0])), unit, g, rows, KP)

        def load_branch(k, passes):
            for g in passes:
                load_w(wpool.tile([P, T, DO], U8, name="wb%d" % g), 2 * k, g, range(T), DO)

        x_sb = keep.tile([P, 2, DI], BF16, name="x_sb")
        wf = keep.tile([P, UNITS, 2 * DO], U8, name="wf", align_bytes=64)
        wfs = keep.tile([P, SCALE_SLOTS, DO], U8, name="wfs", align_bytes=64)
        bf1_b = keep.tile([P, DO], BF16, name="bf1_b")

        load_unit(0, 1, (0, 1))
        load_unit(1, 1, (0, 1))
        load_unit(0, 1, (2, 3))
        load_unit(0, 0)
        load_unit(1, 1, (2, 3))
        nc.sync.dma_start(out=x_sb[:], in_=x.rearrange("(r p) k -> p r k", p=P))
        load_unit(1, 0)
        load_branch(1, (1, 0))

        ident = keep.tile([P, P], F32, name="ident")
        make_identity(nc, ident[:])
        ident16 = keep.tile([P, P], BF16, name="ident16")
        make_identity(nc, ident16[:])
        eps = keep.tile([P, 1], F32, name="eps")
        nc.vector.memset(eps[:], 1.0)
        nc.scalar.activation(eps[:], eps[:], ACT.Abs_reciprocal_sqrt, scale=EPS**-2)
        for slot in range(0, SCALE_SLOTS, 4):
            nc.vector.memset(wfs[:, slot : slot + 4, :].rearrange("p u n -> p (u n)").bitcast(I32), 0)

        def load_scales(unit, units):
            slot = unit % SCALE_SLOTS
            for q in range(4):
                nc.sync.dma_start(
                    out=wfs[32 * q : 32 * q + 4, slot : slot + units].bitcast(I32),
                    in_=Wf1_scales[unit : unit + units, 4 * q : 4 * q + 4, :].rearrange("u q n -> q u n").bitcast(I32),
                )

        for k in range(2, W_BUFS):
            load_branch(k, (0, 1))
        load_scales(0, SCALE_SLOTS)
        for piece in range(4):
            units = slice(4 * piece, 4 * piece + 4)
            nc.sync.dma_start(out=wf[:, units], in_=Wf1_words[units].rearrange("u p n -> p u n"))
            if piece == 0:
                load_branch(W_BUFS, (0, 1))
        nc.sync.dma_start(out=bf1_b[:], in_=bf1.partition_broadcast(P))

        x_codes = keep.tile([P, NG, B], U32, name="x_codes", align_bytes=64)
        x_scales = keep.tile([P, NG, B], U8, name="x_scales", align_bytes=64)
        x_grouped = keep.tile([P, NG, B, T], BF16, name="x_grouped", align_bytes=64)
        shifts = keep.tile([P, 2, UNITS, T], F32, name="shifts")
        gain = keep.tile([P, UNITS, 2, T], F32, name="gain")

        def turn_x():
            x_words = x_sb[:].bitcast(F32)
            for g in range(NG):
                xt = hps.tile([P, 2, 2, P], F32, name="h")
                for r in range(2):
                    for u in range(2):
                        nc.tensor.transpose(xt[:, r, u, :], x_words[:, r, 256 * g + u : 256 * (g + 1) : 2], ident[:])
                on_scalar(x_grouped[:, g].bitcast(F32).rearrange("p (r n) u -> p r n u", r=2), xt[:].rearrange("p r u n -> p r n u"))

        def turn_vectors():
            vt = hps.tile([P, 2, P], F32, name="h")
            for u in range(2):
                nc.tensor.transpose(vt[:, u, :], vrows[:].bitcast(F32)[:, u::2], ident[:])
            values = vt[:].bitcast(BF16).rearrange("p u (r e) -> p r u e", e=2)
            on_scalar(shifts[:].rearrange("p v r (u e) -> p (v r) u e", e=2), values[:, 0 : 2 * UNITS])
            on_scalar(gain[:, :, 0, :].rearrange("p r (u e) -> p r u e", e=2), values[:, 2 * UNITS : 3 * UNITS])

        def quant_x():
            nc.vector.quantize_mx(
                x_codes[:].rearrange("p g n -> p (g n)").bitcast(FP8X4),
                x_scales[:].rearrange("p g n -> p (g n)"),
                x_grouped[:].rearrange("p g n j -> p (g n j)"),
            )

        plane, wide, grouped, woven, codes, scales = ({} for n in range(6))

        def scale_row(dst, i, g, j, units):
            row = wrows[i, g, j][:, 0 : KP * units]
            nc.vector.tensor_scalar(dst, row.bitcast(FP8), kscale[:, g * T + j : g * T + j + 1], None, op0=ALU.mult)

        def widen(i, g, units, rows=range(T), scalar_rows=()):
            if (i, g) not in wide:
                wide[i, g] = work.tile([P, T, DO], BF16, name="plane%d" % g, align_bytes=64)
                for n in range(units):
                    plane[i + n, g] = wide[i, g][:, :, KP * n : KP * (n + 1)]
            tile = wide[i, g]
            for j in rows:
                if j in scalar_rows:
                    row = wrows[i, g, j][:, 0 : KP * units]
                    nc.scalar.activation(tile[:, j, 0 : KP * units], row.bitcast(FP8), ACT.Copy, scale=kscale[:, g * T + j : g * T + j + 1])
                else:
                    scale_row(tile[:, j, 0 : KP * units], i, g, j, units)

        def widen_pairs(i, g, units, rows=EVEN_ROWS + ODD_ROWS):
            if (i, g) not in wide:
                wide[i, g] = work.tile([P, 2, DO, 2], BF16, name="plane%d" % g, align_bytes=64)
                for n in range(units):
                    plane[i + n, g] = wide[i, g][:, :, KP * n : KP * (n + 1), :]
            for j in rows:
                scale_row(wide[i, g][:, j // 2, 0 : KP * units, j % 2], i, g, j, units)

        def group_tile(i, g):
            if i not in grouped:
                grouped[i] = work.tile([P, NG, T, P, T], BF16, name="grouped", align_bytes=64)
            return grouped[i][:, g]

        def lay_out(i, g, m0=0):
            dst = group_tile(i, g)[:, :, m0:P, :].rearrange("p t (q e) j -> p q t j e", e=2)
            on_scalar(dst, plane[i, g][:, :, T * m0 : KP].rearrange("p j (q e t) -> p q t j e", e=2, t=T))

        def merge(i, g):
            dst = group_tile(i, g).bitcast(F32).rearrange("p t m u -> p m t u")
            on_scalar(dst, plane[i, g].bitcast(F32).rearrange("p u (m t) z -> p m t (u z)", t=T))

        def merge_on_vector(i, g):
            dst = group_tile(i, g).bitcast(F32).rearrange("p (s t) m u -> p m s u t", s=2)
            on_vector(dst, plane[i, g].bitcast(F32).rearrange("p u (m s t) z -> p m s u (t z)", s=2, t=2))

        def weave(i, quads=BANK_QUADS):
            for bank in range(2):
                woven[i, bank] = wps.tile([P, 2, T * quads, 2], BF16, name="woven")
            for u in range(2):
                for bank in range(2):
                    rows = plane[i, 1][:, 2 * u : 2 * u + 2, T * quads * bank : T * quads * (bank + 1)]
                    nc.tensor.matmul(
                        woven[i, bank][:, u].rearrange("p (q c) e -> p q e c", c=LINE),
                        lhsT=ident16[:],
                        rhs=rows.rearrange("p e (q c) -> p q e c", c=LINE),
                        start=True,
                        stop=True,
                    )

        def unweave(i, quads=BANK_QUADS):
            for bank in range(2):
                dst = group_tile(i, 1)[:, :, quads * bank : quads * (bank + 1), :].bitcast(F32)
                on_scalar(dst, woven[i, bank][:].bitcast(F32).rearrange("p u (m t) z -> p t m (u z)", t=T))

        def quant(i):
            codes[i] = work.tile([P, NG, KP], U32, name="codes", align_bytes=64)
            scales[i] = work.tile([P, NG, KP], U8, name="scales", align_bytes=64)
            nc.vector.quantize_mx(
                codes[i][:].rearrange("p g c -> p (g c)").bitcast(FP8X4),
                scales[i][:].rearrange("p g c -> p (g c)"),
                grouped[i][:].rearrange("p g t m j -> p (g t m j)"),
            )

        h, a, npairs, fused, fused_codes, fused_scales, both = ({} for n in range(7))
        sums = keep.tile([P, UNITS, T], F32, name="sums")
        squares = keep.tile([P, UNITS, T], F32, name="squares")
        rstd = keep.tile([P, UNITS, 1, T], F32, name="rstd")
        slopes = keep.tile([P, UNITS, 2, T], F32, name="slopes")
        offsets = keep.tile([P, UNITS, T], F32, name="offsets")

        def mm1(i):
            for bank in range(2):
                h[i, bank] = hps.tile([P, 2, B], F32, name="h")
                for t in (2 * bank, 2 * bank + 1):
                    cols = slice(P * t, P * (t + 1))
                    for g in (1, 0):
                        nc.tensor.matmul_mx(
                            h[i, bank][:, t % 2, :],
                            lhsT=codes[i][:, g, cols].bitcast(FP8X4),
                            lhsT_scale=scales[i][:, g, cols],
                            rhs=x_codes[:, g, :].bitcast(FP8X4),
                            rhs_scale=x_scales[:, g, :],
                            start=(g == 1),
                            stop=(g == 0),
                        )

        def relu(i, products=range(T)):
            if i not in a:
                a[i] = apool.tile([P, T, B], F32, name="a")
            for t in products:
                nc.scalar.activation(a[i][:, t, :], h[i, t // 2][:, t % 2, :], ACT.Relu, bias=shifts[:, 0, i, t : t + 1], accum_out=sums[:, i, t : t + 1])

        def square(i):
            terms = work.tile([P, T, B], BF16, name="terms")
            for t in range(T):
                nc.scalar.activation(
                    terms[:, t, :], a[i][:, t, :], ACT.Square, bias=sums[:, i, t : t + 1], scale=-float(B), accum_out=squares[:, i, t : t + 1]
                )

        def root(i, units):
            u = slice(i, i + units)
            nc.scalar.activation(rstd[:, u, 0, :], squares[:, u], ACT.Abs_reciprocal_sqrt, bias=eps[:], scale=1.0 / B**3)

        def centre(i, units):
            u = slice(i, i + units)
            nc.vector.scalar_tensor_tensor(gain[:, u, 1, :], sums[:, u], -1.0 / B, gain[:, u, 0, :], op0=ALU.mult, op1=ALU.mult)

        def slope(i, units):
            u = slice(i, i + units)
            nc.vector.tensor_tensor(slopes[:, u], rstd[:, u].to_broadcast([P, units, 2, T]), gain[:, u], op=ALU.mult)

        def offset(i, units):
            u = slice(i, i + units)
            nc.vector.tensor_tensor(offsets[:, u], slopes[:, u, 1, :], shifts[:, 1, u], op=ALU.add)

        def normalise(dst, i, products, rows):
            for t in products:
                nc.vector.tensor_scalar(
                    dst[:, t // 2, :, t % 2], a[i][:, t, rows], slopes[:, i, 0, t : t + 1], offsets[:, i, t : t + 1], op0=ALU.mult, op1=ALU.add
                )

        def norm(i, products=EVEN_ROWS + ODD_ROWS):
            if i not in npairs:
                npairs[i] = work.tile([P, 2, B, 2], BF16, name="npairs", align_bytes=64)
            normalise(npairs[i], i, products, slice(0, B))

        def norm_both(i):
            for products in (EVEN_ROWS, ODD_ROWS):
                norm(i, products)
                norm(i + 1, products)

        def branch_tiles(i):
            first = i - i % 2
            if first not in both:
                both[first] = (
                    work.tile([P, 2, B, T], BF16, name="fused", align_bytes=64),
                    work.tile([P, 2, B], U32, name="fused_codes", align_bytes=64),
                    work.tile([P, 2, B], U8, name="fused_scales", align_bytes=64),
                )
                for n in range(2):
                    fused[first + n], fused_codes[first + n], fused_scales[first + n] = (tile[:, n] for tile in both[first])

        def nmerge(i, copy):
            branch_tiles(i)
            run = 2 if copy is on_vector else 1
            dst = fused[i].bitcast(F32).rearrange("p (q e) u -> p q u e", e=run)
            copy(dst, npairs[i][:].bitcast(F32).rearrange("p u (q e) z -> p q u (e z)", e=run))

        def nquant(i, rows=slice(0, B)):
            nc.vector.quantize_mx(fused_codes[i][:, rows].bitcast(FP8X4), fused_scales[i][:, rows], fused[i][:, rows].rearrange("p n t -> p (n t)"))

        def nquant_both(i):
            values, words, exponents = both[i]
            nc.vector.quantize_mx(
                words[:].rearrange("p u n -> p (u n)").bitcast(FP8X4),
                exponents[:].rearrange("p u n -> p (u n)"),
                values[:].rearrange("p u n t -> p (u n t)"),
            )

        acc = {}
        for m in range(2):
            for n in range(2):
                acc[m, n] = accps.tile([P, KP], F32, name="acc%d%d" % (m, n))

        def mm2(i, halves=(0, 1)):
            for m in halves:
                rows = slice(P * m, P * (m + 1))
                for n in range(2):
                    nc.tensor.matmul_mx(
                        acc[m, n][:],
                        lhsT=fused_codes[i][:, rows].bitcast(FP8X4),
                        lhsT_scale=fused_scales[i][:, rows],
                        rhs=wf[:, i, DO * n : DO * (n + 1)].bitcast(FP4X4),
                        rhs_scale=wfs[:, i % SCALE_SLOTS, KP * n : KP * (n + 1)],
                        start=(i == 0),
                        stop=(i == LAST),
                    )

        widen_pairs(0, 1, 1)
        widen(1, 1, 1, (0, 1, 2), scalar_rows=(0, 1, 2))
        merge(0, 1)
        turn_vectors()
        widen_pairs(0, 0, 1)
        merge(0, 0)
        widen(1, 1, 1, (3,))
        turn_x()
        weave(1, SPARE_QUADS)
        widen_pairs(1, 0, 1)
        lay_out(1, 1, 2 * SPARE_QUADS)
        merge(1, 0)
        unweave(1, SPARE_QUADS)
        quant(0)
        quant_x()
        mm1(0)
        widen(2, 1, 2)
        weave(2)

        for s in range(2, UNITS - 2, 2):
            first = s == 2
            relu(s - 2)
            if first:
                widen_pairs(s, 0, 1)
            else:
                widen(s, 1, 2)
                weave(s)
            square(s - 2)
            if not first:
                offset(s - 4, 2)
            quant(s - 1)
            mm1(s - 1)
            if s >= 6:
                mm2(s - 5)
            if first:
                unweave(s)
                merge(s, 0)
                widen_pairs(s + 1, 0, 1)
            else:
                merge(s, 0)
                norm_both(s - 4)
                unweave(s)
            ahead = s // 2 + W_BUFS - 1
            if W_BUFS < ahead < NB:
                load_branch(ahead, (0, 1))
            if s >= 8 and s % 4 == 0:
                load_scales(s, 4)

            relu(s - 1)
            weave(s + 1)
            widen_pairs(s + 2, 0, 2, EVEN_ROWS)
            square(s - 1)
            if not first:
                nmerge(s - 4, on_scalar)
                nmerge(s - 3, on_scalar)
            quant(s)
            mm1(s)
            centre(s - 2, 2)
            widen_pairs(s + 2, 0, 2, ODD_ROWS[:1])
            if first:
                merge(s + 1, 0)
            root(s - 2, 2)
            if not first:
                merge(s + 1, 0)
            widen_pairs(s + 2, 0, 2, ODD_ROWS[1:])
            if not first:
                nquant_both(s - 4)
                mm2(s - 4)
            slope(s - 2, 2)
            unweave(s + 1)

        s = UNITS - 2
        widen_pairs(s, 1, 2, EVEN_ROWS)
        mm2(s - 5, (0,))
        relu(s - 2)
        offset(s - 4, 2)
        quant(s - 1)
        mm1(s - 1)
        mm2(s - 5, (1,))
        widen_pairs(s, 1, 2, ODD_ROWS)
        square(s - 2)
        merge(s, 0)
        norm(s - 4, EVEN_ROWS)
        norm(s - 3, EVEN_ROWS)
        merge_on_vector(s, 1)
        norm(s - 4, ODD_ROWS)
        relu(s - 1)
        quant(s)
        mm1(s)
        merge(s + 1, 0)
        merge(s + 1, 1)
        norm(s - 3, ODD_ROWS)
        nmerge(s - 4, on_vector)
        square(s - 1)
        nmerge(s - 3, on_vector)
        centre(s - 2, 2)
        nquant(s - 4)
        quant(s + 1)
        relu(s, (0,))
        root(s - 2, 2)
        relu(s, (1, 2, 3))
        mm1(s + 1)
        mm2(s - 4)
        slope(s - 2, 2)
        square(s)
        nquant(s - 3)
        mm2(s - 3)
        offset(s - 2, 2)
        centre(s, 1)
        norm(s - 2, EVEN_ROWS)
        norm(s - 1, EVEN_ROWS)
        relu(s + 1, (0,))
        root(s, 1)
        relu(s + 1, (1, 2, 3))
        norm(s - 2, ODD_ROWS)
        norm(s - 1, ODD_ROWS)
        square(s + 1)
        nmerge(s - 2, on_vector)
        slope(s, 1)
        nmerge(s - 1, on_vector)
        offset(s, 1)
        nquant(s - 2)
        mm2(s - 2)
        centre(s + 1, 1)
        norm(s)
        root(s + 1, 1)
        nmerge(s, on_scalar)
        slope(s + 1, 1)
        nquant(s - 1)
        mm2(s - 1)
        offset(s + 1, 1)

        halves = [slice(P * m, P * (m + 1)) for m in range(2)]
        for m in range(2):
            last_pairs = keep.tile([P, 2, P, 2], BF16, name="last_pairs%d" % m, align_bytes=64)
            normalise(last_pairs, LAST, EVEN_ROWS + ODD_ROWS, halves[m])
            if m == 0:
                nquant(s)
            on_scalar(fused[LAST][:, halves[m]].bitcast(F32), last_pairs[:].bitcast(F32).rearrange("p u n z -> p n (u z)"))
        for m in range(2):
            mm2(s, (m,))
            nquant(LAST, halves[m])
            mm2(LAST, (m,))

        width = KP // 2
        for m, c0 in [(m, c0) for m in range(2) for c0 in range(0, DO, width)]:
            cols = slice(c0, c0 + width)
            biased = keep.tile([P, width], F32, name="biased%d_%d" % (m, c0))
            nc.vector.tensor_tensor(biased[:], acc[m, c0 // KP][:, c0 % KP : c0 % KP + width], bf1_b[:, cols], op=ALU.add)
            result = keep.tile([P, width], F32, name="result%d_%d" % (m, c0))
            nc.scalar.activation(result[:], biased[:], ACT.Relu)
            queue = nc.scalar if c0 + width == DO and m == 1 else nc.sync
            queue.dma_start(out=out[halves[m], cols], in_=result[:])
